import numpy as np
import ml_dtypes


def mxq(x, axis, fmt="e4m3"):
    dtype, down = {"e4m3": (ml_dtypes.float8_e4m3fn, 7), "e5m2": (ml_dtypes.float8_e5m2, 14)}[fmt]
    v = np.moveaxis(np.asarray(x, np.float32).astype(ml_dtypes.bfloat16).astype(np.float64), axis, -1)
    blocks = v.reshape(v.shape[:-1] + (-1, 32))
    amax = np.abs(blocks).max(-1, keepdims=True)
    byte = np.maximum(np.where(amax > 0, np.frexp(amax)[1] - 1 + 127, 0) - down, 1)
    scale = np.exp2(byte - 127.0)
    codes = (blocks / scale).astype(np.float32).astype(dtype).astype(np.float64)
    return np.moveaxis((codes * scale).reshape(v.shape), -1, axis)


WIDE = False


def mx_kscale(k):
    if not WIDE:
        return np.ones(k)
    levels = np.array([10, -10, 5, -5, 0])
    a = np.random.permutation(np.resize(levels, k // 512 * 4)).reshape(k // 512, 4)
    idx = np.arange(k)
    return np.exp2(a[idx // 512, idx % 128 // 32])


BF16 = ml_dtypes.bfloat16


def bf(x):
    return np.asarray(x, np.float32).astype(BF16)


def f64(x):
    return np.asarray(x).astype(np.float64)


N, NFEAT, NHEADS, NHID, NCLASS = 1024, 512, 4, 128, 128
HF = NHEADS * NHID
P = 0.08


def elu(v):
    return np.where(v > 0, v, np.exp(np.minimum(v, 0.0)) - 1.0)


def setup_inputs():
    t = mx_kscale(N)
    edges = np.random.random((N, N)) < P
    return {"adj": bf(edges * (0.5 + np.random.random((N, N))) * t),
            "h1": bf(np.random.standard_normal((NHEADS, N, NHID)) * 1.2 / np.sqrt(P * N) / t[:, None]),
            "lin_w": bf(np.random.standard_normal((HF, NCLASS)) * 1.5 / np.sqrt(HF)),
            "lin_b": bf(np.random.standard_normal(NCLASS) * 0.3)}


def reference(adj, h1, lin_w, lin_b):
    hp = mxq(f64(adj), 1, "e4m3") @ mxq(f64(h1), 1, "e4m3")
    emb1 = elu(hp).transpose(1, 0, 2).reshape(N, HF)
    scores = (mxq(elu(emb1), 1, "e4m3") @ mxq(f64(lin_w), 0, "e4m3")) + f64(lin_b)
    shifted = scores - scores.max(1, keepdims=True)
    logp = shifted - np.log(np.exp(shifted).sum(1, keepdims=True))
    return logp, emb1, scores

@@ -1,0 +1,248 @@
+from contextlib import ExitStack
+
+import concourse.mybir as mybir
+from concourse.masks import make_identity
+
+F32 = mybir.dt.float32
+BF16 = mybir.dt.bfloat16
+U32 = mybir.dt.uint32
+U8 = mybir.dt.uint8
+FP8X4 = mybir.dt.float8_e4m3fn_x4
+ACT = mybir.ActivationFunctionType
+ALU = mybir.AluOpType
+AXIS = mybir.AxisListType
+
+P = 128
+PACK = 4
+NODES = 1024
+HEADS = 4
+HID = 128
+FEATS = HEADS * HID
+CLASSES = 128
+ROW_TILES = NODES // P
+PASSES = NODES // (P * PACK)
+HALVES = 2
+
+FLOPS = 2 * NODES * NODES * FEATS + 2 * NODES * FEATS * CLASSES
+
+
+def tile_gat_pb_kernel(tc, adj, h1, lin_w, lin_b, out_0, out_1, out_2):
+    nc = tc.nc
+
+    adj_rows = adj.rearrange("(p i) m -> p i m", i=ROW_TILES)
+    h1_rows = h1.rearrange("h (c p e) f -> h p c (e f)", c=PASSES * HALVES, p=P, e=2)
+    w_rows = lin_w.rearrange("(t p) c -> p t c", p=P)
+    logp_rows = out_0.rearrange("(p i) c -> p i c", i=ROW_TILES)
+    emb1_rows = out_1.rearrange("(p i) c -> p i c", i=ROW_TILES)
+    scores_rows = out_2.rearrange("(p i) c -> p i c", i=ROW_TILES)
+
+    with ExitStack() as ctx:
+        keep = ctx.enter_context(tc.tile_pool(name="keep", bufs=1))
+        inputs = ctx.enter_context(tc.tile_pool(name="inputs", bufs=1))
+        ring = ctx.enter_context(tc.tile_pool(name="ring", bufs=3))
+        psum_adj = ctx.enter_context(tc.psum_pool(name="psum_adj", bufs=2))
+        psum_agg = ctx.enter_context(tc.psum_pool(name="psum_agg", bufs=2))
+        psum_elu = ctx.enter_context(tc.psum_pool(name="psum_elu", bufs=1))
+        psum_cls = ctx.enter_context(tc.psum_pool(name="psum_cls", bufs=2))
+
+        identity = keep.tile([P, P], F32)
+        make_identity(nc, identity[:])
+
+        adj_sb = [inputs.tile([P, NODES], BF16, name="adj_sb%d" % i) for i in range(ROW_TILES)]
+        h1_raw = [inputs.tile([P, PASSES, PACK, HID], BF16, name="h1_raw%d" % h) for h in range(HEADS)]
+        w_raw = inputs.tile([P, PACK, CLASSES], BF16)
+        bias = inputs.tile([P, CLASSES], BF16)
+
+        def load_adj(i):
+            nc.sync.dma_start(out=adj_sb[i][:], in_=adj_rows[:, i, :])
+
+        load_adj(0)
+        for h in range(HEADS):
+            nc.sync.dma_start(
+                out=h1_raw[h][:].rearrange("p g (u e) f -> p (g u) (e f)", e=2), in_=h1_rows[h]
+            )
+        load_adj(1)
+        nc.sync.dma_start(out=w_raw[:], in_=w_rows)
+        nc.sync.dma_start(out=bias[:], in_=lin_b.partition_broadcast(P))
+        for i in range(2, ROW_TILES):
+            load_adj(i)
+
+        h1_grouped = keep.tile([P, PASSES, FEATS, PACK], BF16, align_bytes=64)
+        h1_codes = keep.tile([P, PASSES, FEATS], U32, align_bytes=64)
+        h1_scales = keep.tile([P, PASSES, FEATS], U8, align_bytes=64)
+        w_grouped = keep.tile([P, CLASSES, PACK], BF16, align_bytes=64)
+        w_codes = keep.tile([P, CLASSES], U32, align_bytes=64)
+        w_scales = keep.tile([P, CLASSES], U8, align_bytes=64)
+        scores_sb = keep.tile([P, ROW_TILES, CLASSES], F32)
+        logp_sb = keep.tile([P, ROW_TILES, CLASSES], F32)
+        exp_shifted = keep.tile([P, ROW_TILES, CLASSES], F32)
+        neg_max = keep.tile([P, ROW_TILES], F32)
+        exp_sum = keep.tile([P, ROW_TILES], F32)
+        log_sum = keep.tile([P, ROW_TILES], F32)
+        offset = keep.tile([P, ROW_TILES], F32)
+
+        adj_grouped, adj_codes, adj_scales = {}, {}, {}
+        agg, neg, emb1, neg_t, emb1_t, exp_neg, x2, x2_codes, x2_scales, cls = {}, {}, {}, {}, {}, {}, {}, {}, {}, {}
+
+        def prepare_h1(h):
+            cols = slice(h * HID, (h + 1) * HID)
+            nc.vector.tensor_copy(out=h1_grouped[:, 0, cols, :], in_=h1_raw[h][:, 0].rearrange("p t f -> p f t"))
+            nc.scalar.copy(out=h1_grouped[:, 1, cols, :], in_=h1_raw[h][:, 1].rearrange("p t f -> p f t"))
+            for g in range(PASSES):
+                nc.vector.quantize_mx(
+                    out=h1_codes[:, g, cols].bitcast(FP8X4),
+                    scales=h1_scales[:, g, cols],
+                    in_=h1_grouped[:, g, cols, :].rearrange("p f t -> p (f t)"),
+                )
+
+        def prepare_classifier():
+            nc.vector.tensor_copy(out=w_grouped[:], in_=w_raw[:].rearrange("p t c -> p c t"))
+            nc.vector.quantize_mx(
+                out=w_codes[:].bitcast(FP8X4), scales=w_scales[:], in_=w_grouped[:].rearrange("p c t -> p (c t)")
+            )
+
+        def transpose_adj(i):
+            words = adj_sb[i][:].bitcast(F32)
+            adj_t = psum_adj.tile([P, PASSES * HALVES, P], F32)
+            for c in range(PASSES * HALVES):
+                nc.tensor.transpose(adj_t[:, c, :], words[:, c * P : (c + 1) * P], identity[:])
+            adj_grouped[i] = ring.tile([P, PASSES * P * PACK], BF16, name="adj_grouped", align_bytes=64)
+            nc.scalar.copy(
+                out=adj_grouped[i][:].bitcast(F32).rearrange("p (g n u) -> p g n u", g=PASSES, u=HALVES),
+                in_=adj_t[:].rearrange("p (g u) n -> p g n u", u=HALVES),
+            )
+
+        def quantise_adj(i):
+            adj_codes[i] = ring.tile([P, PASSES * P], U32, name="adj_codes", align_bytes=64)
+            adj_scales[i] = ring.tile([P, PASSES * P], U8, name="adj_scales", align_bytes=64)
+            nc.vector.quantize_mx(
+                out=adj_codes[i][:].bitcast(FP8X4), scales=adj_scales[i][:], in_=adj_grouped[i][:]
+            )
+
+        def aggregate(i):
+            agg[i] = psum_agg.tile([P, FEATS], F32, name="agg")
+            for g in range(PASSES):
+                rows = slice(g * P, (g + 1) * P)
+                nc.tensor.matmul_mx(
+                    out=agg[i][:],
+                    lhsT=adj_codes[i][:, rows].bitcast(FP8X4),
+                    lhsT_scale=adj_scales[i][:, rows],
+                    rhs=h1_codes[:, g, :].bitcast(FP8X4),
+                    rhs_scale=h1_scales[:, g, :],
+                    start=(g == 0),
+                    stop=(g == PASSES - 1),
+                )
+
+        def transpose_features(dst, src):
+            for t in range(HEADS):
+                nc.tensor.transpose(dst[:, t, :], src[:, t * HID : (t + 1) * HID], identity[:])
+
+        def first_elu(i):
+            exp_v = ring.tile([P, FEATS], F32, name="exp_v")
+            nc.scalar.activation(out=exp_v[:], in_=agg[i][:], func=ACT.Exp)
+            neg[i] = ring.tile([P, FEATS], F32, name="neg")
+            nc.vector.tensor_scalar(
+                out=neg[i][:], in0=exp_v[:], scalar1=1.0, scalar2=-1.0, op0=ALU.min, op1=ALU.add
+            )
+            neg_t[i] = psum_elu.tile([P, HEADS, P], F32, name="neg_t")
+            transpose_features(neg_t[i], neg[i])
+            emb1[i] = ring.tile([P, FEATS], F32, name="emb1")
+            nc.vector.tensor_tensor(out=emb1[i][:], in0=agg[i][:], in1=neg[i][:], op=ALU.max)
+            nc.sync.dma_start(out=emb1_rows[:, i, :], in_=emb1[i][:])
+            emb1_t[i] = psum_elu.tile([P, HEADS, P], F32, name="emb1_t")
+            transpose_features(emb1_t[i], emb1[i])
+
+        def second_elu_exp(i):
+            exp_neg[i] = ring.tile([P, P, PACK], F32, name="exp_neg")
+            nc.scalar.activation(out=exp_neg[i][:], in_=neg_t[i][:].rearrange("p t n -> p n t"), func=ACT.Exp)
+
+        def second_elu(i):
+            x2[i] = ring.tile([P, P, PACK], BF16, name="x2", align_bytes=64)
+            nc.vector.scalar_tensor_tensor(
+                out=x2[i][:],
+                in0=exp_neg[i][:],
+                scalar=-1.0,
+                in1=emb1_t[i][:].rearrange("p t n -> p n t"),
+                op0=ALU.add,
+                op1=ALU.max,
+            )
+
+        def quantise_x2(i):
+            x2_codes[i] = ring.tile([P, P], U32, name="x2_codes", align_bytes=64)
+            x2_scales[i] = ring.tile([P, P], U8, name="x2_scales", align_bytes=64)
+            nc.vector.quantize_mx(
+                out=x2_codes[i][:].bitcast(FP8X4),
+                scales=x2_scales[i][:],
+                in_=x2[i][:].rearrange("p n t -> p (n t)"),
+            )
+
+        def classify(i):
+            cls[i] = psum_cls.tile([P, CLASSES], F32, name="cls")
+            nc.tensor.matmul_mx(
+                out=cls[i][:],
+                lhsT=x2_codes[i][:].bitcast(FP8X4),
+                lhsT_scale=x2_scales[i][:],
+                rhs=w_codes[:].bitcast(FP8X4),
+                rhs_scale=w_scales[:],
+                start=True,
+                stop=True,
+            )
+
+        def softmax_sums(i):
+            one = slice(i, i + 1)
+            nc.vector.tensor_tensor(out=scores_sb[:, i, :], in0=cls[i][:], in1=bias[:], op=ALU.add)
+            nc.vector.tensor_reduce(
+                out=neg_max[:, one], in_=scores_sb[:, i, :], axis=AXIS.X, op=ALU.max, negate=True
+            )
+            nc.scalar.activation(
+                out=exp_shifted[:, i, :],
+                in_=scores_sb[:, i, :],
+                func=ACT.Exp,
+                bias=neg_max[:, one],
+                scale=1.0,
+                accum_out=exp_sum[:, one],
+            )
+
+        transpose_adj(0)
+        quantise_adj(0)
+        for h in range(HEADS):
+            prepare_h1(h)
+        aggregate(0)
+        transpose_adj(1)
+        quantise_adj(1)
+        aggregate(1)
+        prepare_classifier()
+        transpose_adj(2)
+
+        def in_range(i):
+            return 0 <= i < ROW_TILES
+
+        for s in range(ROW_TILES + 2):
+            if in_range(s):
+                first_elu(s)
+            if in_range(s - 1):
+                quantise_x2(s - 1)
+            if in_range(s + 3):
+                transpose_adj(s + 3)
+            if in_range(s):
+                second_elu_exp(s)
+            if in_range(s - 1):
+                classify(s - 1)
+            if in_range(s - 2):
+                softmax_sums(s - 2)
+            if in_range(s + 2):
+                quantise_adj(s + 2)
+                aggregate(s + 2)
+            if in_range(s):
+                second_elu(s)
+
+        nc.sync.dma_start(out=scores_rows, in_=scores_sb[:])
+        nc.scalar.activation(out=log_sum[:], in_=exp_sum[:], func=ACT.Ln)
+        nc.vector.tensor_tensor(out=offset[:], in0=log_sum[:], in1=neg_max[:], op=ALU.subtract)
+        nc.vector.tensor_tensor(
+            out=logp_sb[:],
+            in0=scores_sb[:],
+            in1=offset[:].unsqueeze(2).to_broadcast([P, ROW_TILES, CLASSES]),
+            op=ALU.subtract,
+        )
+        nc.sync.dma_start(out=logp_rows, in_=logp_sb[:])

@@ -22,6 +22,7 @@ CLASSES = 128
 ROW_TILES = NODES // P
 PASSES = NODES // (P * PACK)
 HALVES = 2
+STORE_GROUP = 4
 
 FLOPS = 2 * NODES * NODES * FEATS + 2 * NODES * FEATS * CLASSES
 
@@ -44,14 +45,19 @@ def tile_gat_pb_kernel(tc, adj, h1, lin_w, lin_b, out_0, out_1, out_2):
         psum_agg = ctx.enter_context(tc.psum_pool(name="psum_agg", bufs=2))
         psum_elu = ctx.enter_context(tc.psum_pool(name="psum_elu", bufs=1))
         psum_cls = ctx.enter_context(tc.psum_pool(name="psum_cls", bufs=2))
+        ctx.enter_context(tc.manual_schedule())
 
         identity = keep.tile([P, P], F32)
         make_identity(nc, identity[:])
+        ones = keep.tile([P, P], BF16)
+        nc.vector.memset(ones[:], 1.0)
+        bias_row = keep.tile([P, CLASSES], BF16)
+        nc.vector.memset(bias_row[:], 0.0)
+        nc.scalar.dma_start(out=bias_row[0:1, :], in_=lin_b.unsqueeze(0))
 
         adj_sb = [inputs.tile([P, NODES], BF16, name="adj_sb%d" % i) for i in range(ROW_TILES)]
         h1_raw = [inputs.tile([P, PASSES, PACK, HID], BF16, name="h1_raw%d" % h) for h in range(HEADS)]
         w_raw = inputs.tile([P, PACK, CLASSES], BF16)
-        bias = inputs.tile([P, CLASSES], BF16)
 
         def load_adj(i):
             nc.sync.dma_start(out=adj_sb[i][:], in_=adj_rows[:, i, :])
@@ -63,7 +69,6 @@ def tile_gat_pb_kernel(tc, adj, h1, lin_w, lin_b, out_0, out_1, out_2):
             )
         load_adj(1)
         nc.sync.dma_start(out=w_raw[:], in_=w_rows)
-        nc.sync.dma_start(out=bias[:], in_=lin_b.partition_broadcast(P))
         for i in range(2, ROW_TILES):
             load_adj(i)
 
@@ -73,6 +78,7 @@ def tile_gat_pb_kernel(tc, adj, h1, lin_w, lin_b, out_0, out_1, out_2):
         w_grouped = keep.tile([P, CLASSES, PACK], BF16, align_bytes=64)
         w_codes = keep.tile([P, CLASSES], U32, align_bytes=64)
         w_scales = keep.tile([P, CLASSES], U8, align_bytes=64)
+        bias = keep.tile([P, CLASSES], F32)
         scores_sb = keep.tile([P, ROW_TILES, CLASSES], F32)
         logp_sb = keep.tile([P, ROW_TILES, CLASSES], F32)
         exp_shifted = keep.tile([P, ROW_TILES, CLASSES], F32)
@@ -81,13 +87,21 @@ def tile_gat_pb_kernel(tc, adj, h1, lin_w, lin_b, out_0, out_1, out_2):
         log_sum = keep.tile([P, ROW_TILES], F32)
         offset = keep.tile([P, ROW_TILES], F32)
 
-        adj_grouped, adj_codes, adj_scales = {}, {}, {}
-        agg, neg, emb1, neg_t, emb1_t, exp_neg, x2, x2_codes, x2_scales, cls = {}, {}, {}, {}, {}, {}, {}, {}, {}, {}
+        adj_t, adj_grouped, adj_codes, adj_scales = {}, {}, {}, {}
+        agg, exp_v, neg, emb1, neg_t, emb1_t, exp_neg, x2, x2_codes, x2_scales, cls = {}, {}, {}, {}, {}, {}, {}, {}, {}, {}, {}
 
-        def prepare_h1(h):
+        def spread_bias():
+            bias_ps = psum_cls.tile([P, CLASSES], F32, name="cls")
+            nc.tensor.matmul(out=bias_ps[:], lhsT=ones[:], rhs=bias_row[:], start=True, stop=True)
+            nc.vector.tensor_copy(out=bias[:], in_=bias_ps[:])
+
+        def regroup_h1(h):
             cols = slice(h * HID, (h + 1) * HID)
             nc.vector.tensor_copy(out=h1_grouped[:, 0, cols, :], in_=h1_raw[h][:, 0].rearrange("p t f -> p f t"))
             nc.scalar.copy(out=h1_grouped[:, 1, cols, :], in_=h1_raw[h][:, 1].rearrange("p t f -> p f t"))
+
+        def quantise_h1(h):
+            cols = slice(h * HID, (h + 1) * HID)
             for g in range(PASSES):
                 nc.vector.quantize_mx(
                     out=h1_codes[:, g, cols].bitcast(FP8X4),
@@ -103,13 +117,15 @@ def tile_gat_pb_kernel(tc, adj, h1, lin_w, lin_b, out_0, out_1, out_2):
 
         def transpose_adj(i):
             words = adj_sb[i][:].bitcast(F32)
-            adj_t = psum_adj.tile([P, PASSES * HALVES, P], F32)
+            adj_t[i] = psum_adj.tile([P, PASSES * HALVES, P], F32, name="adj_t")
             for c in range(PASSES * HALVES):
-                nc.tensor.transpose(adj_t[:, c, :], words[:, c * P : (c + 1) * P], identity[:])
+                nc.tensor.transpose(adj_t[i][:, c, :], words[:, c * P : (c + 1) * P], identity[:])
+
+        def regroup_adj(i):
             adj_grouped[i] = ring.tile([P, PASSES * P * PACK], BF16, name="adj_grouped", align_bytes=64)
             nc.scalar.copy(
                 out=adj_grouped[i][:].bitcast(F32).rearrange("p (g n u) -> p g n u", g=PASSES, u=HALVES),
-                in_=adj_t[:].rearrange("p (g u) n -> p g n u", u=HALVES),
+                in_=adj_t[i][:].rearrange("p (g u) n -> p g n u", u=HALVES),
             )
 
         def quantise_adj(i):
@@ -137,18 +153,24 @@ def tile_gat_pb_kernel(tc, adj, h1, lin_w, lin_b, out_0, out_1, out_2):
             for t in range(HEADS):
                 nc.tensor.transpose(dst[:, t, :], src[:, t * HID : (t + 1) * HID], identity[:])
 
-        def first_elu(i):
-            exp_v = ring.tile([P, FEATS], F32, name="exp_v")
-            nc.scalar.activation(out=exp_v[:], in_=agg[i][:], func=ACT.Exp)
+        def first_elu_exp(i):
+            exp_v[i] = ring.tile([P, FEATS], F32, name="exp_v")
+            nc.scalar.activation(out=exp_v[i][:], in_=agg[i][:], func=ACT.Exp)
+
+        def first_elu_negative(i):
             neg[i] = ring.tile([P, FEATS], F32, name="neg")
             nc.vector.tensor_scalar(
-                out=neg[i][:], in0=exp_v[:], scalar1=1.0, scalar2=-1.0, op0=ALU.min, op1=ALU.add
+                out=neg[i][:], in0=exp_v[i][:], scalar1=1.0, scalar2=-1.0, op0=ALU.min, op1=ALU.add
             )
             neg_t[i] = psum_elu.tile([P, HEADS, P], F32, name="neg_t")
             transpose_features(neg_t[i], neg[i])
+
+        def first_elu(i):
             emb1[i] = ring.tile([P, FEATS], F32, name="emb1")
             nc.vector.tensor_tensor(out=emb1[i][:], in0=agg[i][:], in1=neg[i][:], op=ALU.max)
             nc.sync.dma_start(out=emb1_rows[:, i, :], in_=emb1[i][:])
+
+        def transpose_emb1(i):
             emb1_t[i] = psum_elu.tile([P, HEADS, P], F32, name="emb1_t")
             transpose_features(emb1_t[i], emb1[i])
 
@@ -188,61 +210,83 @@ def tile_gat_pb_kernel(tc, adj, h1, lin_w, lin_b, out_0, out_1, out_2):
                 stop=True,
             )
 
-        def softmax_sums(i):
-            one = slice(i, i + 1)
+        def group_of(i):
+            return slice(i + 1 - STORE_GROUP, i + 1)
+
+        def add_bias_and_max(i):
             nc.vector.tensor_tensor(out=scores_sb[:, i, :], in0=cls[i][:], in1=bias[:], op=ALU.add)
             nc.vector.tensor_reduce(
-                out=neg_max[:, one], in_=scores_sb[:, i, :], axis=AXIS.X, op=ALU.max, negate=True
+                out=neg_max[:, i : i + 1], in_=scores_sb[:, i, :], axis=AXIS.X, op=ALU.max, negate=True
             )
+            if (i + 1) % STORE_GROUP == 0:
+                nc.sync.dma_start(out=scores_rows[:, group_of(i), :], in_=scores_sb[:, group_of(i), :])
+
+        def sum_of_exp(i):
             nc.scalar.activation(
                 out=exp_shifted[:, i, :],
                 in_=scores_sb[:, i, :],
                 func=ACT.Exp,
-                bias=neg_max[:, one],
+                bias=neg_max[:, i : i + 1],
                 scale=1.0,
-                accum_out=exp_sum[:, one],
+                accum_out=exp_sum[:, i : i + 1],
             )
 
+        spread_bias()
         transpose_adj(0)
+        regroup_adj(0)
         quantise_adj(0)
         for h in range(HEADS):
-            prepare_h1(h)
-        aggregate(0)
+            regroup_h1(h)
+            if h > 0:
+                quantise_h1(h - 1)
+        quantise_h1(HEADS - 1)
         transpose_adj(1)
+        regroup_adj(1)
+        aggregate(0)
         quantise_adj(1)
-        aggregate(1)
-        prepare_classifier()
         transpose_adj(2)
+        prepare_classifier()
 
         def in_range(i):
             return 0 <= i < ROW_TILES
 
-        for s in range(ROW_TILES + 2):
+        for s in range(ROW_TILES + 4):
+            if in_range(s - 2):
+                quantise_x2(s - 2)
+            if in_range(s + 1):
+                aggregate(s + 1)
+            if in_range(s - 2):
+                classify(s - 2)
+            if in_range(s - 3):
+                add_bias_and_max(s - 3)
             if in_range(s):
-                first_elu(s)
+                first_elu_exp(s)
             if in_range(s - 1):
-                quantise_x2(s - 1)
+                second_elu_exp(s - 1)
             if in_range(s + 3):
                 transpose_adj(s + 3)
+            if in_range(s + 2):
+                regroup_adj(s + 2)
+            if in_range(s - 3):
+                sum_of_exp(s - 3)
             if in_range(s):
-                second_elu_exp(s)
+                first_elu_negative(s)
+                first_elu(s)
             if in_range(s - 1):
-                classify(s - 1)
-            if in_range(s - 2):
-                softmax_sums(s - 2)
+                second_elu(s - 1)
+            if in_range(s):
+                transpose_emb1(s)
             if in_range(s + 2):
                 quantise_adj(s + 2)
-                aggregate(s + 2)
-            if in_range(s):
-                second_elu(s)
 
-        nc.sync.dma_start(out=scores_rows, in_=scores_sb[:])
         nc.scalar.activation(out=log_sum[:], in_=exp_sum[:], func=ACT.Ln)
         nc.vector.tensor_tensor(out=offset[:], in0=log_sum[:], in1=neg_max[:], op=ALU.subtract)
-        nc.vector.tensor_tensor(
-            out=logp_sb[:],
-            in0=scores_sb[:],
-            in1=offset[:].unsqueeze(2).to_broadcast([P, ROW_TILES, CLASSES]),
-            op=ALU.subtract,
-        )
-        nc.sync.dma_start(out=logp_rows, in_=logp_sb[:])
+        for last in range(STORE_GROUP - 1, ROW_TILES, STORE_GROUP):
+            tiles = group_of(last)
+            nc.vector.tensor_tensor(
+                out=logp_sb[:, tiles, :],
+                in0=scores_sb[:, tiles, :],
+                in1=offset[:, tiles].unsqueeze(2).to_broadcast([P, STORE_GROUP, CLASSES]),
+                op=ALU.subtract,
+            )
+            nc.sync.dma_start(out=logp_rows[:, tiles, :], in_=logp_sb[:, tiles, :])

@@ -43,8 +43,9 @@ def tile_gat_pb_kernel(tc, adj, h1, lin_w, lin_b, out_0, out_1, out_2):
         ring = ctx.enter_context(tc.tile_pool(name="ring", bufs=3))
         psum_adj = ctx.enter_context(tc.psum_pool(name="psum_adj", bufs=2))
         psum_agg = ctx.enter_context(tc.psum_pool(name="psum_agg", bufs=2))
-        psum_elu = ctx.enter_context(tc.psum_pool(name="psum_elu", bufs=1))
-        psum_cls = ctx.enter_context(tc.psum_pool(name="psum_cls", bufs=2))
+        psum_agg_t = ctx.enter_context(tc.psum_pool(name="psum_agg_t", bufs=2))
+        psum_neg_t = ctx.enter_context(tc.psum_pool(name="psum_neg_t", bufs=1))
+        psum_cls = ctx.enter_context(tc.psum_pool(name="psum_cls", bufs=1))
         ctx.enter_context(tc.manual_schedule())
 
         identity = keep.tile([P, P], F32)
@@ -88,7 +89,7 @@ def tile_gat_pb_kernel(tc, adj, h1, lin_w, lin_b, out_0, out_1, out_2):
         offset = keep.tile([P, ROW_TILES], F32)
 
         adj_t, adj_grouped, adj_codes, adj_scales = {}, {}, {}, {}
-        agg, exp_v, neg, emb1, neg_t, emb1_t, exp_neg, x2, x2_codes, x2_scales, cls = {}, {}, {}, {}, {}, {}, {}, {}, {}, {}, {}
+        agg, agg_t, exp_v, neg, emb1, neg_t, exp_neg, x2, x2_codes, x2_scales, cls = {}, {}, {}, {}, {}, {}, {}, {}, {}, {}, {}
 
         def spread_bias():
             bias_ps = psum_cls.tile([P, CLASSES], F32, name="cls")
@@ -149,9 +150,21 @@ def tile_gat_pb_kernel(tc, adj, h1, lin_w, lin_b, out_0, out_1, out_2):
                     stop=(g == PASSES - 1),
                 )
 
-        def transpose_features(dst, src):
+        def aggregate_transposed(i):
+            agg_t[i] = psum_agg_t.tile([P, HEADS, P], F32, name="agg_t")
             for t in range(HEADS):
-                nc.tensor.transpose(dst[:, t, :], src[:, t * HID : (t + 1) * HID], identity[:])
+                cols = slice(t * HID, (t + 1) * HID)
+                for g in range(PASSES):
+                    rows = slice(g * P, (g + 1) * P)
+                    nc.tensor.matmul_mx(
+                        out=agg_t[i][:, t, :],
+                        lhsT=h1_codes[:, g, cols].bitcast(FP8X4),
+                        lhsT_scale=h1_scales[:, g, cols],
+                        rhs=adj_codes[i][:, rows].bitcast(FP8X4),
+                        rhs_scale=adj_scales[i][:, rows],
+                        start=(g == 0),
+                        stop=(g == PASSES - 1),
+                    )
 
         def first_elu_exp(i):
             exp_v[i] = ring.tile([P, FEATS], F32, name="exp_v")
@@ -162,17 +175,14 @@ def tile_gat_pb_kernel(tc, adj, h1, lin_w, lin_b, out_0, out_1, out_2):
             nc.vector.tensor_scalar(
                 out=neg[i][:], in0=exp_v[i][:], scalar1=1.0, scalar2=-1.0, op0=ALU.min, op1=ALU.add
             )
-            neg_t[i] = psum_elu.tile([P, HEADS, P], F32, name="neg_t")
-            transpose_features(neg_t[i], neg[i])
+            neg_t[i] = psum_neg_t.tile([P, HEADS, P], F32, name="neg_t")
+            for t in range(HEADS):
+                nc.tensor.transpose(neg_t[i][:, t, :], neg[i][:, t * HID : (t + 1) * HID], identity[:])
 
         def first_elu(i):
             emb1[i] = ring.tile([P, FEATS], F32, name="emb1")
             nc.vector.tensor_tensor(out=emb1[i][:], in0=agg[i][:], in1=neg[i][:], op=ALU.max)
             nc.sync.dma_start(out=emb1_rows[:, i, :], in_=emb1[i][:])
-
-        def transpose_emb1(i):
-            emb1_t[i] = psum_elu.tile([P, HEADS, P], F32, name="emb1_t")
-            transpose_features(emb1_t[i], emb1[i])
 
         def second_elu_exp(i):
             exp_neg[i] = ring.tile([P, P, PACK], F32, name="exp_neg")
@@ -184,7 +194,7 @@ def tile_gat_pb_kernel(tc, adj, h1, lin_w, lin_b, out_0, out_1, out_2):
                 out=x2[i][:],
                 in0=exp_neg[i][:],
                 scalar=-1.0,
-                in1=emb1_t[i][:].rearrange("p t n -> p n t"),
+                in1=agg_t[i][:].rearrange("p t n -> p n t"),
                 op0=ALU.add,
                 op1=ALU.max,
             )
@@ -231,7 +241,6 @@ def tile_gat_pb_kernel(tc, adj, h1, lin_w, lin_b, out_0, out_1, out_2):
                 accum_out=exp_sum[:, i : i + 1],
             )
 
-        spread_bias()
         transpose_adj(0)
         regroup_adj(0)
         quantise_adj(0)
@@ -246,6 +255,7 @@ def tile_gat_pb_kernel(tc, adj, h1, lin_w, lin_b, out_0, out_1, out_2):
         quantise_adj(1)
         transpose_adj(2)
         prepare_classifier()
+        spread_bias()
 
         def in_range(i):
             return 0 <= i < ROW_TILES
@@ -253,12 +263,14 @@ def tile_gat_pb_kernel(tc, adj, h1, lin_w, lin_b, out_0, out_1, out_2):
         for s in range(ROW_TILES + 4):
             if in_range(s - 2):
                 quantise_x2(s - 2)
-            if in_range(s + 1):
-                aggregate(s + 1)
-            if in_range(s - 2):
-                classify(s - 2)
             if in_range(s - 3):
                 add_bias_and_max(s - 3)
+            if in_range(s + 1):
+                aggregate(s + 1)
+            if in_range(s):
+                aggregate_transposed(s)
+            if in_range(s - 2):
+                classify(s - 2)
             if in_range(s):
                 first_elu_exp(s)
             if in_range(s - 1):
@@ -274,8 +286,6 @@ def tile_gat_pb_kernel(tc, adj, h1, lin_w, lin_b, out_0, out_1, out_2):
                 first_elu(s)
             if in_range(s - 1):
                 second_elu(s - 1)
-            if in_range(s):
-                transpose_emb1(s)
             if in_range(s + 2):
                 quantise_adj(s + 2)
 

@@ -223,13 +223,15 @@ def tile_gat_pb_kernel(tc, adj, h1, lin_w, lin_b, out_0, out_1, out_2):
         def group_of(i):
             return slice(i + 1 - STORE_GROUP, i + 1)
 
-        def add_bias_and_max(i):
+        def add_bias(i):
             nc.vector.tensor_tensor(out=scores_sb[:, i, :], in0=cls[i][:], in1=bias[:], op=ALU.add)
+            if (i + 1) % STORE_GROUP == 0:
+                nc.sync.dma_start(out=scores_rows[:, group_of(i), :], in_=scores_sb[:, group_of(i), :])
+
+        def negative_max(i):
             nc.vector.tensor_reduce(
                 out=neg_max[:, i : i + 1], in_=scores_sb[:, i, :], axis=AXIS.X, op=ALU.max, negate=True
             )
-            if (i + 1) % STORE_GROUP == 0:
-                nc.sync.dma_start(out=scores_rows[:, group_of(i), :], in_=scores_sb[:, group_of(i), :])
 
         def sum_of_exp(i):
             nc.scalar.activation(
@@ -243,51 +245,49 @@ def tile_gat_pb_kernel(tc, adj, h1, lin_w, lin_b, out_0, out_1, out_2):
 
         transpose_adj(0)
         regroup_adj(0)
+        regroup_h1(0)
         quantise_adj(0)
-        for h in range(HEADS):
+        for h in range(1, HEADS):
             regroup_h1(h)
-            if h > 0:
-                quantise_h1(h - 1)
+            quantise_h1(h - 1)
         quantise_h1(HEADS - 1)
         transpose_adj(1)
         regroup_adj(1)
-        aggregate(0)
-        quantise_adj(1)
-        transpose_adj(2)
         prepare_classifier()
         spread_bias()
 
         def in_range(i):
             return 0 <= i < ROW_TILES
 
-        for s in range(ROW_TILES + 4):
+        for s in range(-2, ROW_TILES + 3):
             if in_range(s - 2):
                 quantise_x2(s - 2)
             if in_range(s - 3):
-                add_bias_and_max(s - 3)
+                add_bias(s - 3)
             if in_range(s + 1):
-                aggregate(s + 1)
-            if in_range(s):
-                aggregate_transposed(s)
-            if in_range(s - 2):
-                classify(s - 2)
-            if in_range(s):
-                first_elu_exp(s)
-            if in_range(s - 1):
-                second_elu_exp(s - 1)
-            if in_range(s + 3):
-                transpose_adj(s + 3)
-            if in_range(s + 2):
-                regroup_adj(s + 2)
-            if in_range(s - 3):
-                sum_of_exp(s - 3)
+                first_elu_exp(s + 1)
             if in_range(s):
                 first_elu_negative(s)
-                first_elu(s)
+            if in_range(s + 4):
+                transpose_adj(s + 4)
+            if in_range(s - 3):
+                negative_max(s - 3)
+                sum_of_exp(s - 3)
+            if in_range(s - 2):
+                classify(s - 2)
             if in_range(s - 1):
                 second_elu(s - 1)
+            if in_range(s + 1):
+                aggregate_transposed(s + 1)
+            if in_range(s):
+                second_elu_exp(s)
+                first_elu(s)
             if in_range(s + 2):
-                quantise_adj(s + 2)
+                aggregate(s + 2)
+            if in_range(s + 4):
+                regroup_adj(s + 4)
+            if in_range(s + 3):
+                quantise_adj(s + 3)
 
         nc.scalar.activation(out=log_sum[:], in_=exp_sum[:], func=ACT.Ln)
         nc.vector.tensor_tensor(out=offset[:], in0=log_sum[:], in1=neg_max[:], op=ALU.subtract)

@@ -23,6 +23,7 @@ ROW_TILES = NODES // P
 PASSES = NODES // (P * PACK)
 HALVES = 2
 STORE_GROUP = 4
+RUN = 4
 
 FLOPS = 2 * NODES * NODES * FEATS + 2 * NODES * FEATS * CLASSES
 
@@ -69,8 +70,9 @@ def tile_gat_pb_kernel(tc, adj, h1, lin_w, lin_b, out_0, out_1, out_2):
                 out=h1_raw[h][:].rearrange("p g (u e) f -> p (g u) (e f)", e=2), in_=h1_rows[h]
             )
         load_adj(1)
+        load_adj(2)
         nc.sync.dma_start(out=w_raw[:], in_=w_rows)
-        for i in range(2, ROW_TILES):
+        for i in range(3, ROW_TILES):
             load_adj(i)
 
         h1_grouped = keep.tile([P, PASSES, FEATS, PACK], BF16, align_bytes=64)
@@ -86,7 +88,6 @@ def tile_gat_pb_kernel(tc, adj, h1, lin_w, lin_b, out_0, out_1, out_2):
         neg_max = keep.tile([P, ROW_TILES], F32)
         exp_sum = keep.tile([P, ROW_TILES], F32)
         log_sum = keep.tile([P, ROW_TILES], F32)
-        offset = keep.tile([P, ROW_TILES], F32)
 
         adj_t, adj_grouped, adj_codes, adj_scales = {}, {}, {}, {}
         agg, agg_t, exp_v, neg, emb1, neg_t, exp_neg, x2, x2_codes, x2_scales, cls = {}, {}, {}, {}, {}, {}, {}, {}, {}, {}, {}
@@ -96,10 +97,16 @@ def tile_gat_pb_kernel(tc, adj, h1, lin_w, lin_b, out_0, out_1, out_2):
             nc.tensor.matmul(out=bias_ps[:], lhsT=ones[:], rhs=bias_row[:], start=True, stop=True)
             nc.vector.tensor_copy(out=bias[:], in_=bias_ps[:])
 
+        def to_words(grouped):
+            return grouped.rearrange("p (c i) t -> p c t i", i=RUN)
+
+        def from_rows(raw):
+            return raw.rearrange("p t (c i) -> p c t i", i=RUN)
+
         def regroup_h1(h):
             cols = slice(h * HID, (h + 1) * HID)
-            nc.vector.tensor_copy(out=h1_grouped[:, 0, cols, :], in_=h1_raw[h][:, 0].rearrange("p t f -> p f t"))
-            nc.scalar.copy(out=h1_grouped[:, 1, cols, :], in_=h1_raw[h][:, 1].rearrange("p t f -> p f t"))
+            nc.vector.tensor_copy(out=to_words(h1_grouped[:, 0, cols, :]), in_=from_rows(h1_raw[h][:, 0]))
+            nc.scalar.copy(out=to_words(h1_grouped[:, 1, cols, :]), in_=from_rows(h1_raw[h][:, 1]))
 
         def quantise_h1(h):
             cols = slice(h * HID, (h + 1) * HID)
@@ -111,7 +118,7 @@ def tile_gat_pb_kernel(tc, adj, h1, lin_w, lin_b, out_0, out_1, out_2):
                 )
 
         def prepare_classifier():
-            nc.vector.tensor_copy(out=w_grouped[:], in_=w_raw[:].rearrange("p t c -> p c t"))
+            nc.vector.tensor_copy(out=to_words(w_grouped[:]), in_=from_rows(w_raw[:]))
             nc.vector.quantize_mx(
                 out=w_codes[:].bitcast(FP8X4), scales=w_scales[:], in_=w_grouped[:].rearrange("p c t -> p (c t)")
             )
@@ -290,13 +297,14 @@ def tile_gat_pb_kernel(tc, adj, h1, lin_w, lin_b, out_0, out_1, out_2):
                 quantise_adj(s + 3)
 
         nc.scalar.activation(out=log_sum[:], in_=exp_sum[:], func=ACT.Ln)
-        nc.vector.tensor_tensor(out=offset[:], in0=log_sum[:], in1=neg_max[:], op=ALU.subtract)
-        for last in range(STORE_GROUP - 1, ROW_TILES, STORE_GROUP):
-            tiles = group_of(last)
-            nc.vector.tensor_tensor(
-                out=logp_sb[:, tiles, :],
-                in0=scores_sb[:, tiles, :],
-                in1=offset[:, tiles].unsqueeze(2).to_broadcast([P, STORE_GROUP, CLASSES]),
-                op=ALU.subtract,
+        for i in range(ROW_TILES):
+            nc.vector.tensor_scalar(
+                out=logp_sb[:, i, :],
+                in0=scores_sb[:, i, :],
+                scalar1=neg_max[:, i : i + 1],
+                scalar2=log_sum[:, i : i + 1],
+                op0=ALU.add,
+                op1=ALU.subtract,
             )
-            nc.sync.dma_start(out=logp_rows[:, tiles, :], in_=logp_sb[:, tiles, :])
+            if (i + 1) % STORE_GROUP == 0:
+                nc.sync.dma_start(out=logp_rows[:, group_of(i), :], in_=logp_sb[:, group_of(i), :])

@@ -19,6 +19,7 @@ HEADS = 4
 HID = 128
 FEATS = HEADS * HID
 CLASSES = 128
+COPIES = 4
 ROW_TILES = NODES // P
 PASSES = NODES // (P * PACK)
 HALVES = 2
@@ -33,7 +34,7 @@ def tile_gat_pb_kernel(tc, adj, h1, lin_w, lin_b, out_0, out_1, out_2):
 
     adj_rows = adj.rearrange("(p i) m -> p i m", i=ROW_TILES)
     h1_rows = h1.rearrange("h (c p e) f -> h p c (e f)", c=PASSES * HALVES, p=P, e=2)
-    w_rows = lin_w.rearrange("(t p) c -> p t c", p=P)
+    w_rows = lin_w.rearrange("(u p e) c -> p u (e c)", u=HALVES, e=2)
     logp_rows = out_0.rearrange("(p i) c -> p i c", i=ROW_TILES)
     emb1_rows = out_1.rearrange("(p i) c -> p i c", i=ROW_TILES)
     scores_rows = out_2.rearrange("(p i) c -> p i c", i=ROW_TILES)
@@ -41,11 +42,10 @@ def tile_gat_pb_kernel(tc, adj, h1, lin_w, lin_b, out_0, out_1, out_2):
     with ExitStack() as ctx:
         keep = ctx.enter_context(tc.tile_pool(name="keep", bufs=1))
         inputs = ctx.enter_context(tc.tile_pool(name="inputs", bufs=1))
-        ring = ctx.enter_context(tc.tile_pool(name="ring", bufs=3))
+        ring = ctx.enter_context(tc.tile_pool(name="ring", bufs=4))
         psum_adj = ctx.enter_context(tc.psum_pool(name="psum_adj", bufs=2))
-        psum_agg = ctx.enter_context(tc.psum_pool(name="psum_agg", bufs=2))
-        psum_agg_t = ctx.enter_context(tc.psum_pool(name="psum_agg_t", bufs=2))
-        psum_neg_t = ctx.enter_context(tc.psum_pool(name="psum_neg_t", bufs=1))
+        psum_agg = ctx.enter_context(tc.psum_pool(name="psum_agg", bufs=4))
+        psum_x2 = ctx.enter_context(tc.psum_pool(name="psum_x2", bufs=1))
         psum_cls = ctx.enter_context(tc.psum_pool(name="psum_cls", bufs=1))
         ctx.enter_context(tc.manual_schedule())
 
@@ -53,6 +53,8 @@ def tile_gat_pb_kernel(tc, adj, h1, lin_w, lin_b, out_0, out_1, out_2):
         make_identity(nc, identity[:])
         ones = keep.tile([P, P], BF16)
         nc.vector.memset(ones[:], 1.0)
+        zeros = keep.tile([P, COPIES * CLASSES], BF16)
+        nc.gpsimd.memset(zeros[:], 0.0)
         bias_row = keep.tile([P, CLASSES], BF16)
         nc.vector.memset(bias_row[:], 0.0)
         nc.scalar.dma_start(out=bias_row[0:1, :], in_=lin_b.unsqueeze(0))
@@ -64,14 +66,19 @@ def tile_gat_pb_kernel(tc, adj, h1, lin_w, lin_b, out_0, out_1, out_2):
         def load_adj(i):
             nc.sync.dma_start(out=adj_sb[i][:], in_=adj_rows[:, i, :])
 
-        load_adj(0)
-        for h in range(HEADS):
+        def load_h1(h):
             nc.sync.dma_start(
                 out=h1_raw[h][:].rearrange("p g (u e) f -> p (g u) (e f)", e=2), in_=h1_rows[h]
             )
+
+        load_h1(0)
+        load_h1(1)
+        load_h1(2)
+        load_adj(0)
+        load_h1(3)
         load_adj(1)
         load_adj(2)
-        nc.sync.dma_start(out=w_raw[:], in_=w_rows)
+        nc.sync.dma_start(out=w_raw[:].rearrange("p (u e) c -> p u (e c)", e=2), in_=w_rows)
         for i in range(3, ROW_TILES):
             load_adj(i)
 
@@ -79,8 +86,8 @@ def tile_gat_pb_kernel(tc, adj, h1, lin_w, lin_b, out_0, out_1, out_2):
         h1_codes = keep.tile([P, PASSES, FEATS], U32, align_bytes=64)
         h1_scales = keep.tile([P, PASSES, FEATS], U8, align_bytes=64)
         w_grouped = keep.tile([P, CLASSES, PACK], BF16, align_bytes=64)
-        w_codes = keep.tile([P, CLASSES], U32, align_bytes=64)
-        w_scales = keep.tile([P, CLASSES], U8, align_bytes=64)
+        w_codes = keep.tile([P, COPIES, CLASSES], U32, align_bytes=64)
+        w_scales = keep.tile([P, COPIES, CLASSES], U8, align_bytes=64)
         bias = keep.tile([P, CLASSES], F32)
         scores_sb = keep.tile([P, ROW_TILES, CLASSES], F32)
         logp_sb = keep.tile([P, ROW_TILES, CLASSES], F32)
@@ -90,12 +97,19 @@ def tile_gat_pb_kernel(tc, adj, h1, lin_w, lin_b, out_0, out_1, out_2):
         log_sum = keep.tile([P, ROW_TILES], F32)
 
         adj_t, adj_grouped, adj_codes, adj_scales = {}, {}, {}, {}
-        agg, agg_t, exp_v, neg, emb1, neg_t, exp_neg, x2, x2_codes, x2_scales, cls = {}, {}, {}, {}, {}, {}, {}, {}, {}, {}, {}
+        agg, exp_v, neg, emb1, exp_neg, x2, x2_t, x2_grouped, x2_codes, x2_scales, cls = {}, {}, {}, {}, {}, {}, {}, {}, {}, {}, {}
 
         def spread_bias():
-            bias_ps = psum_cls.tile([P, CLASSES], F32, name="cls")
-            nc.tensor.matmul(out=bias_ps[:], lhsT=ones[:], rhs=bias_row[:], start=True, stop=True)
-            nc.vector.tensor_copy(out=bias[:], in_=bias_ps[:])
+            cls[0] = psum_cls.tile([P, COPIES * CLASSES], F32, name="cls")
+            nc.tensor.matmul(out=cls[0][:, :CLASSES], lhsT=ones[:], rhs=bias_row[:], start=True, stop=True)
+
+        def copy_bias():
+            nc.vector.tensor_copy(out=bias[:], in_=cls[0][:, :CLASSES])
+
+        def warm_up(n):
+            warm_ps = psum_agg.tile([P, FEATS], F32, name="agg")
+            for j in range(n):
+                nc.tensor.matmul(out=warm_ps[:], lhsT=ones[:], rhs=zeros[:], start=True, stop=True)
 
         def to_words(grouped):
             return grouped.rearrange("p (c i) t -> p c t i", i=RUN)
@@ -103,25 +117,30 @@ def tile_gat_pb_kernel(tc, adj, h1, lin_w, lin_b, out_0, out_1, out_2):
         def from_rows(raw):
             return raw.rearrange("p t (c i) -> p c t i", i=RUN)
 
-        def regroup_h1(h):
+        def regroup_h1_pass(h, g, copy):
             cols = slice(h * HID, (h + 1) * HID)
-            nc.vector.tensor_copy(out=to_words(h1_grouped[:, 0, cols, :]), in_=from_rows(h1_raw[h][:, 0]))
-            nc.scalar.copy(out=to_words(h1_grouped[:, 1, cols, :]), in_=from_rows(h1_raw[h][:, 1]))
+            copy(out=to_words(h1_grouped[:, g, cols, :]), in_=from_rows(h1_raw[h][:, g]))
 
-        def quantise_h1(h):
+        def quantise_h1_pass(h, g):
             cols = slice(h * HID, (h + 1) * HID)
-            for g in range(PASSES):
-                nc.vector.quantize_mx(
-                    out=h1_codes[:, g, cols].bitcast(FP8X4),
-                    scales=h1_scales[:, g, cols],
-                    in_=h1_grouped[:, g, cols, :].rearrange("p f t -> p (f t)"),
-                )
+            nc.vector.quantize_mx(
+                out=h1_codes[:, g, cols].bitcast(FP8X4),
+                scales=h1_scales[:, g, cols],
+                in_=h1_grouped[:, g, cols, :].rearrange("p f t -> p (f t)"),
+            )
 
         def prepare_classifier():
             nc.vector.tensor_copy(out=to_words(w_grouped[:]), in_=from_rows(w_raw[:]))
+
+        def quantise_w():
             nc.vector.quantize_mx(
-                out=w_codes[:].bitcast(FP8X4), scales=w_scales[:], in_=w_grouped[:].rearrange("p c t -> p (c t)")
+                out=w_codes[:, 0, :].bitcast(FP8X4),
+                scales=w_scales[:, 0, :],
+                in_=w_grouped[:].rearrange("p c t -> p (c t)"),
             )
+            for c in range(1, COPIES):
+                nc.gpsimd.tensor_copy(out=w_codes[:, c, :], in_=w_codes[:, 0, :])
+                nc.gpsimd.tensor_copy(out=w_scales[:, c, :], in_=w_scales[:, 0, :])
 
         def transpose_adj(i):
             words = adj_sb[i][:].bitcast(F32)
@@ -129,9 +148,9 @@ def tile_gat_pb_kernel(tc, adj, h1, lin_w, lin_b, out_0, out_1, out_2):
             for c in range(PASSES * HALVES):
                 nc.tensor.transpose(adj_t[i][:, c, :], words[:, c * P : (c + 1) * P], identity[:])
 
-        def regroup_adj(i):
+        def regroup_adj(i, copy=nc.scalar.copy):
             adj_grouped[i] = ring.tile([P, PASSES * P * PACK], BF16, name="adj_grouped", align_bytes=64)
-            nc.scalar.copy(
+            copy(
                 out=adj_grouped[i][:].bitcast(F32).rearrange("p (g n u) -> p g n u", g=PASSES, u=HALVES),
                 in_=adj_t[i][:].rearrange("p (g u) n -> p g n u", u=HALVES),
             )
@@ -157,22 +176,6 @@ def tile_gat_pb_kernel(tc, adj, h1, lin_w, lin_b, out_0, out_1, out_2):
                     stop=(g == PASSES - 1),
                 )
 
-        def aggregate_transposed(i):
-            agg_t[i] = psum_agg_t.tile([P, HEADS, P], F32, name="agg_t")
-            for t in range(HEADS):
-                cols = slice(t * HID, (t + 1) * HID)
-                for g in range(PASSES):
-                    rows = slice(g * P, (g + 1) * P)
-                    nc.tensor.matmul_mx(
-                        out=agg_t[i][:, t, :],
-                        lhsT=h1_codes[:, g, cols].bitcast(FP8X4),
-                        lhsT_scale=h1_scales[:, g, cols],
-                        rhs=adj_codes[i][:, rows].bitcast(FP8X4),
-                        rhs_scale=adj_scales[i][:, rows],
-                        start=(g == 0),
-                        stop=(g == PASSES - 1),
-                    )
-
         def first_elu_exp(i):
             exp_v[i] = ring.tile([P, FEATS], F32, name="exp_v")
             nc.scalar.activation(out=exp_v[i][:], in_=agg[i][:], func=ACT.Exp)
@@ -182,9 +185,6 @@ def tile_gat_pb_kernel(tc, adj, h1, lin_w, lin_b, out_0, out_1, out_2):
             nc.vector.tensor_scalar(
                 out=neg[i][:], in0=exp_v[i][:], scalar1=1.0, scalar2=-1.0, op0=ALU.min, op1=ALU.add
             )
-            neg_t[i] = psum_neg_t.tile([P, HEADS, P], F32, name="neg_t")
-            for t in range(HEADS):
-                nc.tensor.transpose(neg_t[i][:, t, :], neg[i][:, t * HID : (t + 1) * HID], identity[:])
 
         def first_elu(i):
             emb1[i] = ring.tile([P, FEATS], F32, name="emb1")
@@ -192,18 +192,26 @@ def tile_gat_pb_kernel(tc, adj, h1, lin_w, lin_b, out_0, out_1, out_2):
             nc.sync.dma_start(out=emb1_rows[:, i, :], in_=emb1[i][:])
 
         def second_elu_exp(i):
-            exp_neg[i] = ring.tile([P, P, PACK], F32, name="exp_neg")
-            nc.scalar.activation(out=exp_neg[i][:], in_=neg_t[i][:].rearrange("p t n -> p n t"), func=ACT.Exp)
+            exp_neg[i] = ring.tile([P, FEATS], F32, name="exp_neg")
+            nc.scalar.activation(out=exp_neg[i][:], in_=neg[i][:], func=ACT.Exp)
 
         def second_elu(i):
-            x2[i] = ring.tile([P, P, PACK], BF16, name="x2", align_bytes=64)
+            x2[i] = ring.tile([P, FEATS], BF16, name="x2")
             nc.vector.scalar_tensor_tensor(
-                out=x2[i][:],
-                in0=exp_neg[i][:],
-                scalar=-1.0,
-                in1=agg_t[i][:].rearrange("p t n -> p n t"),
-                op0=ALU.add,
-                op1=ALU.max,
+                out=x2[i][:], in0=exp_neg[i][:], scalar=-1.0, in1=agg[i][:], op0=ALU.add, op1=ALU.max
+            )
+
+        def transpose_x2(i):
+            words = x2[i][:].bitcast(F32)
+            x2_t[i] = psum_x2.tile([P, HALVES, P], F32, name="x2_t")
+            for u in range(HALVES):
+                nc.tensor.transpose(x2_t[i][:, u, :], words[:, u * P : (u + 1) * P], identity[:])
+
+        def regroup_x2(i):
+            x2_grouped[i] = ring.tile([P, P * PACK], BF16, name="x2_grouped", align_bytes=64)
+            nc.scalar.copy(
+                out=x2_grouped[i][:].bitcast(F32).rearrange("p (n u) -> p n u", u=HALVES),
+                in_=x2_t[i][:].rearrange("p u n -> p n u"),
             )
 
         def quantise_x2(i):
@@ -212,17 +220,18 @@ def tile_gat_pb_kernel(tc, adj, h1, lin_w, lin_b, out_0, out_1, out_2):
             nc.vector.quantize_mx(
                 out=x2_codes[i][:].bitcast(FP8X4),
                 scales=x2_scales[i][:],
-                in_=x2[i][:].rearrange("p n t -> p (n t)"),
+                in_=x2_grouped[i][:],
             )
 
         def classify(i):
-            cls[i] = psum_cls.tile([P, CLASSES], F32, name="cls")
+            width = CLASSES if i >= ROW_TILES - 2 else COPIES * CLASSES
+            cls[i] = psum_cls.tile([P, COPIES * CLASSES], F32, name="cls")
             nc.tensor.matmul_mx(
-                out=cls[i][:],
+                out=cls[i][:, :width],
                 lhsT=x2_codes[i][:].bitcast(FP8X4),
                 lhsT_scale=x2_scales[i][:],
-                rhs=w_codes[:].bitcast(FP8X4),
-                rhs_scale=w_scales[:],
+                rhs=w_codes[:].rearrange("p k c -> p (k c)")[:, :width].bitcast(FP8X4),
+                rhs_scale=w_scales[:].rearrange("p k c -> p (k c)")[:, :width],
                 start=True,
                 stop=True,
             )
@@ -231,7 +240,7 @@ def tile_gat_pb_kernel(tc, adj, h1, lin_w, lin_b, out_0, out_1, out_2):
             return slice(i + 1 - STORE_GROUP, i + 1)
 
         def add_bias(i):
-            nc.vector.tensor_tensor(out=scores_sb[:, i, :], in0=cls[i][:], in1=bias[:], op=ALU.add)
+            nc.vector.tensor_tensor(out=scores_sb[:, i, :], in0=cls[i][:, :CLASSES], in1=bias[:], op=ALU.add)
             if (i + 1) % STORE_GROUP == 0:
                 nc.sync.dma_start(out=scores_rows[:, group_of(i), :], in_=scores_sb[:, group_of(i), :])
 
@@ -250,52 +259,78 @@ def tile_gat_pb_kernel(tc, adj, h1, lin_w, lin_b, out_0, out_1, out_2):
                 accum_out=exp_sum[:, i : i + 1],
             )
 
+
+        on_vector, on_scalar = nc.vector.tensor_copy, nc.scalar.copy
+        warm_up(4)
+        spread_bias()
+        warm_up(2)
+        for h in range(2):
+            regroup_h1_pass(h, 0, on_vector)
+            regroup_h1_pass(h, 1, on_scalar)
+        regroup_h1_pass(2, 1, on_scalar)
+        quantise_h1_pass(0, 0)
+        quantise_h1_pass(1, 0)
+        quantise_h1_pass(0, 1)
+        regroup_h1_pass(2, 0, on_vector)
+        quantise_h1_pass(1, 1)
         transpose_adj(0)
         regroup_adj(0)
-        regroup_h1(0)
+        regroup_h1_pass(3, 0, on_vector)
+        regroup_h1_pass(3, 1, on_vector)
+        quantise_h1_pass(2, 0)
+        quantise_h1_pass(3, 0)
         quantise_adj(0)
-        for h in range(1, HEADS):
-            regroup_h1(h)
-            quantise_h1(h - 1)
-        quantise_h1(HEADS - 1)
+        quantise_h1_pass(2, 1)
+        quantise_h1_pass(3, 1)
         transpose_adj(1)
         regroup_adj(1)
+        transpose_adj(2)
         prepare_classifier()
-        spread_bias()
+        copy_bias()
 
         def in_range(i):
             return 0 <= i < ROW_TILES
 
-        for s in range(-2, ROW_TILES + 3):
-            if in_range(s - 2):
-                quantise_x2(s - 2)
+        late = (6, 7)
+        for s in range(-3, ROW_TILES + 5):
             if in_range(s - 3):
                 add_bias(s - 3)
-            if in_range(s + 1):
-                first_elu_exp(s + 1)
+            if in_range(s - 1):
+                regroup_x2(s - 1)
             if in_range(s):
-                first_elu_negative(s)
-            if in_range(s + 4):
-                transpose_adj(s + 4)
-            if in_range(s - 3):
-                negative_max(s - 3)
-                sum_of_exp(s - 3)
+                second_elu(s)
+            if in_range(s + 1):
+                second_elu_exp(s + 1)
+            if in_range(s - 4):
+                negative_max(s - 4)
+            if in_range(s + 5):
+                regroup_adj(s + 5)
             if in_range(s - 2):
                 classify(s - 2)
-            if in_range(s - 1):
-                second_elu(s - 1)
-            if in_range(s + 1):
-                aggregate_transposed(s + 1)
-            if in_range(s):
-                second_elu_exp(s)
-                first_elu(s)
-            if in_range(s + 2):
-                aggregate(s + 2)
-            if in_range(s + 4):
-                regroup_adj(s + 4)
             if in_range(s + 3):
-                quantise_adj(s + 3)
-
+                aggregate(s + 3)
+            if in_range(s + 6):
+                transpose_adj(s + 6)
+            if in_range(s + 4):
+                quantise_adj(s + 4)
+            if in_range(s + 1) and s + 1 not in late:
+                first_elu(s + 1)
+            if s == ROW_TILES:
+                first_elu(6)
+            if s == ROW_TILES + 3:
+                first_elu(7)
+            if in_range(s):
+                transpose_x2(s)
+            if in_range(s - 1):
+                quantise_x2(s - 1)
+            if in_range(s + 3):
+                first_elu_exp(s + 3)
+            if in_range(s + 2):
+                first_elu_negative(s + 2)
+            if in_range(s - 5):
+                sum_of_exp(s - 5)
+            if s == -2:
+                quantise_w()
         nc.scalar.activation(out=log_sum[:], in_=exp_sum[:], func=ACT.Ln)
         for i in range(ROW_TILES):
             nc.vector.tensor_scalar(

@@ -19,7 +19,6 @@ HEADS = 4
 HID = 128
 FEATS = HEADS * HID
 CLASSES = 128
-COPIES = 4
 ROW_TILES = NODES // P
 PASSES = NODES // (P * PACK)
 HALVES = 2
@@ -53,7 +52,7 @@ def tile_gat_pb_kernel(tc, adj, h1, lin_w, lin_b, out_0, out_1, out_2):
         make_identity(nc, identity[:])
         ones = keep.tile([P, P], BF16)
         nc.vector.memset(ones[:], 1.0)
-        zeros = keep.tile([P, COPIES * CLASSES], BF16)
+        zeros = keep.tile([P, FEATS], BF16)
         nc.gpsimd.memset(zeros[:], 0.0)
         bias_row = keep.tile([P, CLASSES], BF16)
         nc.vector.memset(bias_row[:], 0.0)
@@ -86,8 +85,8 @@ def tile_gat_pb_kernel(tc, adj, h1, lin_w, lin_b, out_0, out_1, out_2):
         h1_codes = keep.tile([P, PASSES, FEATS], U32, align_bytes=64)
         h1_scales = keep.tile([P, PASSES, FEATS], U8, align_bytes=64)
         w_grouped = keep.tile([P, CLASSES, PACK], BF16, align_bytes=64)
-        w_codes = keep.tile([P, COPIES, CLASSES], U32, align_bytes=64)
-        w_scales = keep.tile([P, COPIES, CLASSES], U8, align_bytes=64)
+        w_codes = keep.tile([P, CLASSES], U32, align_bytes=64)
+        w_scales = keep.tile([P, CLASSES], U8, align_bytes=64)
         bias = keep.tile([P, CLASSES], F32)
         scores_sb = keep.tile([P, ROW_TILES, CLASSES], F32)
         logp_sb = keep.tile([P, ROW_TILES, CLASSES], F32)
@@ -100,11 +99,11 @@ def tile_gat_pb_kernel(tc, adj, h1, lin_w, lin_b, out_0, out_1, out_2):
         agg, exp_v, neg, emb1, exp_neg, x2, x2_t, x2_grouped, x2_codes, x2_scales, cls = {}, {}, {}, {}, {}, {}, {}, {}, {}, {}, {}
 
         def spread_bias():
-            cls[0] = psum_cls.tile([P, COPIES * CLASSES], F32, name="cls")
-            nc.tensor.matmul(out=cls[0][:, :CLASSES], lhsT=ones[:], rhs=bias_row[:], start=True, stop=True)
+            cls[0] = psum_cls.tile([P, CLASSES], F32, name="cls")
+            nc.tensor.matmul(out=cls[0][:], lhsT=ones[:], rhs=bias_row[:], start=True, stop=True)
 
         def copy_bias():
-            nc.vector.tensor_copy(out=bias[:], in_=cls[0][:, :CLASSES])
+            nc.vector.tensor_copy(out=bias[:], in_=cls[0][:])
 
         def warm_up(n):
             warm_ps = psum_agg.tile([P, FEATS], F32, name="agg")
@@ -134,13 +133,8 @@ def tile_gat_pb_kernel(tc, adj, h1, lin_w, lin_b, out_0, out_1, out_2):
 
         def quantise_w():
             nc.vector.quantize_mx(
-                out=w_codes[:, 0, :].bitcast(FP8X4),
-                scales=w_scales[:, 0, :],
-                in_=w_grouped[:].rearrange("p c t -> p (c t)"),
+                out=w_codes[:].bitcast(FP8X4), scales=w_scales[:], in_=w_grouped[:].rearrange("p c t -> p (c t)")
             )
-            for c in range(1, COPIES):
-                nc.gpsimd.tensor_copy(out=w_codes[:, c, :], in_=w_codes[:, 0, :])
-                nc.gpsimd.tensor_copy(out=w_scales[:, c, :], in_=w_scales[:, 0, :])
 
         def transpose_adj(i):
             words = adj_sb[i][:].bitcast(F32)
@@ -164,7 +158,7 @@ def tile_gat_pb_kernel(tc, adj, h1, lin_w, lin_b, out_0, out_1, out_2):
 
         def aggregate(i):
             agg[i] = psum_agg.tile([P, FEATS], F32, name="agg")
-            for g in range(PASSES):
+            for g, start, stop in ((0, True, False), (1, False, True)):
                 rows = slice(g * P, (g + 1) * P)
                 nc.tensor.matmul_mx(
                     out=agg[i][:],
@@ -172,8 +166,8 @@ def tile_gat_pb_kernel(tc, adj, h1, lin_w, lin_b, out_0, out_1, out_2):
                     lhsT_scale=adj_scales[i][:, rows],
                     rhs=h1_codes[:, g, :].bitcast(FP8X4),
                     rhs_scale=h1_scales[:, g, :],
-                    start=(g == 0),
-                    stop=(g == PASSES - 1),
+                    start=start,
+                    stop=stop,
                 )
 
         def first_elu_exp(i):
@@ -203,7 +197,17 @@ def tile_gat_pb_kernel(tc, adj, h1, lin_w, lin_b, out_0, out_1, out_2):
 
         def transpose_x2(i):
             words = x2[i][:].bitcast(F32)
-            x2_t[i] = psum_x2.tile([P, HALVES, P], F32, name="x2_t")
+            x2_t[i] = psum_x2.tile([P, PACK, P], F32, name="x2_t")
+            if i < 0:
+                nc.tensor.matmul_mx(
+                    out=x2_t[i][:].rearrange("p a n -> p (a n)"),
+                    lhsT=h1_codes[:, 0, :P].bitcast(FP8X4),
+                    lhsT_scale=h1_scales[:, 0, :P],
+                    rhs=h1_codes[:, 0, :].bitcast(FP8X4),
+                    rhs_scale=h1_scales[:, 0, :],
+                    start=True,
+                    stop=True,
+                )
             for u in range(HALVES):
                 nc.tensor.transpose(x2_t[i][:, u, :], words[:, u * P : (u + 1) * P], identity[:])
 
@@ -211,7 +215,7 @@ def tile_gat_pb_kernel(tc, adj, h1, lin_w, lin_b, out_0, out_1, out_2):
             x2_grouped[i] = ring.tile([P, P * PACK], BF16, name="x2_grouped", align_bytes=64)
             nc.scalar.copy(
                 out=x2_grouped[i][:].bitcast(F32).rearrange("p (n u) -> p n u", u=HALVES),
-                in_=x2_t[i][:].rearrange("p u n -> p n u"),
+                in_=x2_t[i][:, :HALVES, :].rearrange("p u n -> p n u"),
             )
 
         def quantise_x2(i):
@@ -224,14 +228,13 @@ def tile_gat_pb_kernel(tc, adj, h1, lin_w, lin_b, out_0, out_1, out_2):
             )
 
         def classify(i):
-            width = CLASSES if i >= ROW_TILES - 2 else COPIES * CLASSES
-            cls[i] = psum_cls.tile([P, COPIES * CLASSES], F32, name="cls")
+            cls[i] = psum_cls.tile([P, CLASSES], F32, name="cls")
             nc.tensor.matmul_mx(
-                out=cls[i][:, :width],
+                out=cls[i][:],
                 lhsT=x2_codes[i][:].bitcast(FP8X4),
                 lhsT_scale=x2_scales[i][:],
-                rhs=w_codes[:].rearrange("p k c -> p (k c)")[:, :width].bitcast(FP8X4),
-                rhs_scale=w_scales[:].rearrange("p k c -> p (k c)")[:, :width],
+                rhs=w_codes[:].bitcast(FP8X4),
+                rhs_scale=w_scales[:],
                 start=True,
                 stop=True,
             )
@@ -240,7 +243,7 @@ def tile_gat_pb_kernel(tc, adj, h1, lin_w, lin_b, out_0, out_1, out_2):
             return slice(i + 1 - STORE_GROUP, i + 1)
 
         def add_bias(i):
-            nc.vector.tensor_tensor(out=scores_sb[:, i, :], in0=cls[i][:, :CLASSES], in1=bias[:], op=ALU.add)
+            nc.vector.tensor_tensor(out=scores_sb[:, i, :], in0=cls[i][:], in1=bias[:], op=ALU.add)
             if (i + 1) % STORE_GROUP == 0:
                 nc.sync.dma_start(out=scores_rows[:, group_of(i), :], in_=scores_sb[:, group_of(i), :])
 
@@ -261,7 +264,7 @@ def tile_gat_pb_kernel(tc, adj, h1, lin_w, lin_b, out_0, out_1, out_2):
 
 
         on_vector, on_scalar = nc.vector.tensor_copy, nc.scalar.copy
-        warm_up(4)
+        warm_up(1)
         spread_bias()
         warm_up(2)
         for h in range(2):
@@ -274,6 +277,7 @@ def tile_gat_pb_kernel(tc, adj, h1, lin_w, lin_b, out_0, out_1, out_2):
         regroup_h1_pass(2, 0, on_vector)
         quantise_h1_pass(1, 1)
         transpose_adj(0)
+        warm_up(2)
         regroup_adj(0)
         regroup_h1_pass(3, 0, on_vector)
         regroup_h1_pass(3, 1, on_vector)
@@ -283,6 +287,7 @@ def tile_gat_pb_kernel(tc, adj, h1, lin_w, lin_b, out_0, out_1, out_2):
         quantise_h1_pass(2, 1)
         quantise_h1_pass(3, 1)
         transpose_adj(1)
+        warm_up(1)
         regroup_adj(1)
         transpose_adj(2)
         prepare_classifier()

@@ -32,7 +32,7 @@ def tile_gat_pb_kernel(tc, adj, h1, lin_w, lin_b, out_0, out_1, out_2):
     nc = tc.nc
 
     adj_rows = adj.rearrange("(p i) m -> p i m", i=ROW_TILES)
-    h1_rows = h1.rearrange("h (c p e) f -> h p c (e f)", c=PASSES * HALVES, p=P, e=2)
+    h1_rows = h1.rearrange("h (g p t) f -> h p g (t f)", g=PASSES, p=P, t=PACK)
     w_rows = lin_w.rearrange("(u p e) c -> p u (e c)", u=HALVES, e=2)
     logp_rows = out_0.rearrange("(p i) c -> p i c", i=ROW_TILES)
     emb1_rows = out_1.rearrange("(p i) c -> p i c", i=ROW_TILES)
@@ -67,7 +67,7 @@ def tile_gat_pb_kernel(tc, adj, h1, lin_w, lin_b, out_0, out_1, out_2):
 
         def load_h1(h):
             nc.sync.dma_start(
-                out=h1_raw[h][:].rearrange("p g (u e) f -> p (g u) (e f)", e=2), in_=h1_rows[h]
+                out=h1_raw[h][:].rearrange("p g t f -> p g (t f)"), in_=h1_rows[h]
             )
 
         load_h1(0)
@@ -139,8 +139,10 @@ def tile_gat_pb_kernel(tc, adj, h1, lin_w, lin_b, out_0, out_1, out_2):
         def transpose_adj(i):
             words = adj_sb[i][:].bitcast(F32)
             adj_t[i] = psum_adj.tile([P, PASSES * HALVES, P], F32, name="adj_t")
-            for c in range(PASSES * HALVES):
-                nc.tensor.transpose(adj_t[i][:, c, :], words[:, c * P : (c + 1) * P], identity[:])
+            for g in range(PASSES):
+                for u in range(HALVES):
+                    half = words[:, HALVES * g * P + u : HALVES * (g + 1) * P : HALVES]
+                    nc.tensor.transpose(adj_t[i][:, HALVES * g + u, :], half, identity[:])
 
         def regroup_adj(i, copy=nc.scalar.copy):
             adj_grouped[i] = ring.tile([P, PASSES * P * PACK], BF16, name="adj_grouped", align_bytes=64)
@@ -198,7 +200,7 @@ def tile_gat_pb_kernel(tc, adj, h1, lin_w, lin_b, out_0, out_1, out_2):
         def transpose_x2(i):
             words = x2[i][:].bitcast(F32)
             x2_t[i] = psum_x2.tile([P, PACK, P], F32, name="x2_t")
-            if i < 0:
+            if i < 5:
                 nc.tensor.matmul_mx(
                     out=x2_t[i][:].rearrange("p a n -> p (a n)"),
                     lhsT=h1_codes[:, 0, :P].bitcast(FP8X4),
@@ -264,9 +266,7 @@ def tile_gat_pb_kernel(tc, adj, h1, lin_w, lin_b, out_0, out_1, out_2):
 
 
         on_vector, on_scalar = nc.vector.tensor_copy, nc.scalar.copy
-        warm_up(1)
-        spread_bias()
-        warm_up(2)
+        warm_up(4)
         for h in range(2):
             regroup_h1_pass(h, 0, on_vector)
             regroup_h1_pass(h, 1, on_scalar)
@@ -287,16 +287,15 @@ def tile_gat_pb_kernel(tc, adj, h1, lin_w, lin_b, out_0, out_1, out_2):
         quantise_h1_pass(2, 1)
         quantise_h1_pass(3, 1)
         transpose_adj(1)
-        warm_up(1)
         regroup_adj(1)
         transpose_adj(2)
+        aggregate(0)
         prepare_classifier()
-        copy_bias()
 
         def in_range(i):
             return 0 <= i < ROW_TILES
 
-        late = (6, 7)
+        late = (4, 5, 6, 7)
         for s in range(-3, ROW_TILES + 5):
             if in_range(s - 3):
                 add_bias(s - 3)
@@ -312,7 +311,7 @@ def tile_gat_pb_kernel(tc, adj, h1, lin_w, lin_b, out_0, out_1, out_2):
                 regroup_adj(s + 5)
             if in_range(s - 2):
                 classify(s - 2)
-            if in_range(s + 3):
+            if 1 <= s + 3 < ROW_TILES:
                 aggregate(s + 3)
             if in_range(s + 6):
                 transpose_adj(s + 6)
@@ -321,8 +320,11 @@ def tile_gat_pb_kernel(tc, adj, h1, lin_w, lin_b, out_0, out_1, out_2):
             if in_range(s + 1) and s + 1 not in late:
                 first_elu(s + 1)
             if s == ROW_TILES:
-                first_elu(6)
+                first_elu(4)
+            if s == ROW_TILES + 1:
+                first_elu(5)
             if s == ROW_TILES + 3:
+                first_elu(6)
                 first_elu(7)
             if in_range(s):
                 transpose_x2(s)
@@ -335,7 +337,10 @@ def tile_gat_pb_kernel(tc, adj, h1, lin_w, lin_b, out_0, out_1, out_2):
             if in_range(s - 5):
                 sum_of_exp(s - 5)
             if s == -2:
+                spread_bias()
                 quantise_w()
+            if s == -1:
+                copy_bias()
         nc.scalar.activation(out=log_sum[:], in_=exp_sum[:], func=ACT.Ln)
         for i in range(ROW_TILES):
             nc.vector.tensor_scalar(

@@ -77,8 +77,9 @@ def tile_gat_pb_kernel(tc, adj, h1, lin_w, lin_b, out_0, out_1, out_2):
         load_h1(3)
         load_adj(1)
         load_adj(2)
+        load_adj(3)
         nc.sync.dma_start(out=w_raw[:].rearrange("p (u e) c -> p u (e c)", e=2), in_=w_rows)
-        for i in range(3, ROW_TILES):
+        for i in range(4, ROW_TILES):
             load_adj(i)
 
         h1_grouped = keep.tile([P, PASSES, FEATS, PACK], BF16, align_bytes=64)
@@ -91,6 +92,7 @@ def tile_gat_pb_kernel(tc, adj, h1, lin_w, lin_b, out_0, out_1, out_2):
         scores_sb = keep.tile([P, ROW_TILES, CLASSES], F32)
         logp_sb = keep.tile([P, ROW_TILES, CLASSES], F32)
         exp_shifted = keep.tile([P, ROW_TILES, CLASSES], F32)
+        shifted = keep.tile([P, ROW_TILES, CLASSES], F32)
         neg_max = keep.tile([P, ROW_TILES], F32)
         exp_sum = keep.tile([P, ROW_TILES], F32)
         log_sum = keep.tile([P, ROW_TILES], F32)
@@ -144,9 +146,9 @@ def tile_gat_pb_kernel(tc, adj, h1, lin_w, lin_b, out_0, out_1, out_2):
                     half = words[:, HALVES * g * P + u : HALVES * (g + 1) * P : HALVES]
                     nc.tensor.transpose(adj_t[i][:, HALVES * g + u, :], half, identity[:])
 
-        def regroup_adj(i, copy=nc.scalar.copy):
+        def regroup_adj(i):
             adj_grouped[i] = ring.tile([P, PASSES * P * PACK], BF16, name="adj_grouped", align_bytes=64)
-            copy(
+            nc.scalar.copy(
                 out=adj_grouped[i][:].bitcast(F32).rearrange("p (g n u) -> p g n u", g=PASSES, u=HALVES),
                 in_=adj_t[i][:].rearrange("p (g u) n -> p g n u", u=HALVES),
             )
@@ -199,17 +201,10 @@ def tile_gat_pb_kernel(tc, adj, h1, lin_w, lin_b, out_0, out_1, out_2):
 
         def transpose_x2(i):
             words = x2[i][:].bitcast(F32)
-            x2_t[i] = psum_x2.tile([P, PACK, P], F32, name="x2_t")
-            if i < 5:
-                nc.tensor.matmul_mx(
-                    out=x2_t[i][:].rearrange("p a n -> p (a n)"),
-                    lhsT=h1_codes[:, 0, :P].bitcast(FP8X4),
-                    lhsT_scale=h1_scales[:, 0, :P],
-                    rhs=h1_codes[:, 0, :].bitcast(FP8X4),
-                    rhs_scale=h1_scales[:, 0, :],
-                    start=True,
-                    stop=True,
-                )
+            if i == ROW_TILES - 1:
+                x2_t[i] = psum_adj.tile([P, PASSES * HALVES, P], F32, name="adj_t")
+            else:
+                x2_t[i] = psum_x2.tile([P, HALVES, P], F32, name="x2_t")
             for u in range(HALVES):
                 nc.tensor.transpose(x2_t[i][:, u, :], words[:, u * P : (u + 1) * P], identity[:])
 
@@ -290,66 +285,79 @@ def tile_gat_pb_kernel(tc, adj, h1, lin_w, lin_b, out_0, out_1, out_2):
         regroup_adj(1)
         transpose_adj(2)
         aggregate(0)
-        prepare_classifier()
 
         def in_range(i):
             return 0 <= i < ROW_TILES
 
-        late = (4, 5, 6, 7)
-        for s in range(-3, ROW_TILES + 5):
-            if in_range(s - 3):
-                add_bias(s - 3)
-            if in_range(s - 1):
-                regroup_x2(s - 1)
-            if in_range(s):
-                second_elu(s)
+        for s in range(-3, ROW_TILES + 7):
             if in_range(s + 1):
-                second_elu_exp(s + 1)
+                first_elu_negative(s + 1)
+            if in_range(s - 2):
+                quantise_x2(s - 2)
             if in_range(s - 4):
                 negative_max(s - 4)
-            if in_range(s + 5):
-                regroup_adj(s + 5)
+            if in_range(s):
+                second_elu(s)
+            if in_range(s - 7):
+                sum_of_exp(s - 7)
+            if in_range(s + 2):
+                first_elu_exp(s + 2)
+            if 3 <= s + 5 < ROW_TILES:
+                transpose_adj(s + 5)
             if in_range(s - 2):
                 classify(s - 2)
-            if 1 <= s + 3 < ROW_TILES:
-                aggregate(s + 3)
-            if in_range(s + 6):
-                transpose_adj(s + 6)
+            if in_range(s - 1):
+                regroup_x2(s - 1)
             if in_range(s + 4):
                 quantise_adj(s + 4)
-            if in_range(s + 1) and s + 1 not in late:
+            if in_range(s + 1) and s + 1 < 4:
                 first_elu(s + 1)
             if s == ROW_TILES:
                 first_elu(4)
-            if s == ROW_TILES + 1:
-                first_elu(5)
-            if s == ROW_TILES + 3:
-                first_elu(6)
-                first_elu(7)
-            if in_range(s):
-                transpose_x2(s)
-            if in_range(s - 1):
-                quantise_x2(s - 1)
-            if in_range(s + 3):
-                first_elu_exp(s + 3)
-            if in_range(s + 2):
-                first_elu_negative(s + 2)
-            if in_range(s - 5):
-                sum_of_exp(s - 5)
             if s == -2:
                 spread_bias()
+            if 1 <= s + 3 < ROW_TILES:
+                aggregate(s + 3)
+            if in_range(s + 1):
+                second_elu_exp(s + 1)
+            if in_range(s):
+                transpose_x2(s)
+            if s == -2:
+                prepare_classifier()
                 quantise_w()
-            if s == -1:
+            if s == 0:
                 copy_bias()
-        nc.scalar.activation(out=log_sum[:], in_=exp_sum[:], func=ACT.Ln)
-        for i in range(ROW_TILES):
+            if in_range(s - 2):
+                add_bias(s - 2)
+            if s == ROW_TILES + 4:
+                for i in range(4 + 1, ROW_TILES):
+                    first_elu(i)
+            if 2 <= s + 5 < ROW_TILES:
+                regroup_adj(s + 5)
+
+        inverse_sum = keep.tile([P, ROW_TILES], F32)
+        neg_log_sum = keep.tile([P, ROW_TILES], F32)
+        nc.vector.reciprocal(out=inverse_sum[:], in_=exp_sum[:])
+        for i in range(5, ROW_TILES):
+            nc.vector.tensor_scalar(
+                out=shifted[:, i, :], in0=scores_sb[:, i, :], scalar1=neg_max[:, i : i + 1], scalar2=None, op0=ALU.add
+            )
+        nc.scalar.activation(out=neg_log_sum[:], in_=inverse_sum[:], func=ACT.Ln)
+        for i in range(5, ROW_TILES):
+            nc.scalar.activation(
+                out=logp_sb[:, i, :], in_=shifted[:, i, :], func=ACT.Identity, bias=neg_log_sum[:, i : i + 1]
+            )
+        for i in range(5):
             nc.vector.tensor_scalar(
                 out=logp_sb[:, i, :],
                 in0=scores_sb[:, i, :],
                 scalar1=neg_max[:, i : i + 1],
-                scalar2=log_sum[:, i : i + 1],
+                scalar2=neg_log_sum[:, i : i + 1],
                 op0=ALU.add,
-                op1=ALU.subtract,
+                op1=ALU.add,
             )
-            if (i + 1) % STORE_GROUP == 0:
-                nc.sync.dma_start(out=logp_rows[:, group_of(i), :], in_=logp_sb[:, group_of(i), :])
+            if i == 1:
+                nc.sync.dma_start(out=logp_rows[:, 0:2, :], in_=logp_sb[:, 0:2, :])
+            if i == 4:
+                nc.sync.dma_start(out=logp_rows[:, 2:5, :], in_=logp_sb[:, 2:5, :])
+        nc.sync.dma_start(out=logp_rows[:, 5:, :], in_=logp_sb[:, 5:, :])

@@ -56,7 +56,6 @@ def tile_gat_pb_kernel(tc, adj, h1, lin_w, lin_b, out_0, out_1, out_2):
         nc.gpsimd.memset(zeros[:], 0.0)
         bias_row = keep.tile([P, CLASSES], BF16)
         nc.vector.memset(bias_row[:], 0.0)
-        nc.scalar.dma_start(out=bias_row[0:1, :], in_=lin_b.unsqueeze(0))
 
         adj_sb = [inputs.tile([P, NODES], BF16, name="adj_sb%d" % i) for i in range(ROW_TILES)]
         h1_raw = [inputs.tile([P, PASSES, PACK, HID], BF16, name="h1_raw%d" % h) for h in range(HEADS)]
@@ -81,6 +80,8 @@ def tile_gat_pb_kernel(tc, adj, h1, lin_w, lin_b, out_0, out_1, out_2):
         nc.sync.dma_start(out=w_raw[:].rearrange("p (u e) c -> p u (e c)", e=2), in_=w_rows)
         for i in range(4, ROW_TILES):
             load_adj(i)
+            if i == 5:
+                nc.sync.dma_start(out=bias_row[0:1, :], in_=lin_b.unsqueeze(0))
 
         h1_grouped = keep.tile([P, PASSES, FEATS, PACK], BF16, align_bytes=64)
         h1_codes = keep.tile([P, PASSES, FEATS], U32, align_bytes=64)
@@ -95,7 +96,6 @@ def tile_gat_pb_kernel(tc, adj, h1, lin_w, lin_b, out_0, out_1, out_2):
         shifted = keep.tile([P, ROW_TILES, CLASSES], F32)
         neg_max = keep.tile([P, ROW_TILES], F32)
         exp_sum = keep.tile([P, ROW_TILES], F32)
-        log_sum = keep.tile([P, ROW_TILES], F32)
 
         adj_t, adj_grouped, adj_codes, adj_scales = {}, {}, {}, {}
         agg, exp_v, neg, emb1, exp_neg, x2, x2_t, x2_grouped, x2_codes, x2_scales, cls = {}, {}, {}, {}, {}, {}, {}, {}, {}, {}, {}
@@ -314,7 +314,7 @@ def tile_gat_pb_kernel(tc, adj, h1, lin_w, lin_b, out_0, out_1, out_2):
                 first_elu(s + 1)
             if s == ROW_TILES:
                 first_elu(4)
-            if s == -2:
+            if s == 1:
                 spread_bias()
             if 1 <= s + 3 < ROW_TILES:
                 aggregate(s + 3)
@@ -325,7 +325,7 @@ def tile_gat_pb_kernel(tc, adj, h1, lin_w, lin_b, out_0, out_1, out_2):
             if s == -2:
                 prepare_classifier()
                 quantise_w()
-            if s == 0:
+            if s == 1:
                 copy_bias()
             if in_range(s - 2):
                 add_bias(s - 2)

@@ -96,16 +96,18 @@ def tile_gat_pb_kernel(tc, adj, h1, lin_w, lin_b, out_0, out_1, out_2):
         shifted = keep.tile([P, ROW_TILES, CLASSES], F32)
         neg_max = keep.tile([P, ROW_TILES], F32)
         exp_sum = keep.tile([P, ROW_TILES], F32)
+        inverse_sum = keep.tile([P, ROW_TILES], F32)
+        neg_log_sum = keep.tile([P, ROW_TILES], F32)
 
         adj_t, adj_grouped, adj_codes, adj_scales = {}, {}, {}, {}
         agg, exp_v, neg, emb1, exp_neg, x2, x2_t, x2_grouped, x2_codes, x2_scales, cls = {}, {}, {}, {}, {}, {}, {}, {}, {}, {}, {}
 
         def spread_bias():
-            cls[0] = psum_cls.tile([P, CLASSES], F32, name="cls")
-            nc.tensor.matmul(out=cls[0][:], lhsT=ones[:], rhs=bias_row[:], start=True, stop=True)
+            cls[0] = psum_cls.tile([P, CLASSES], F32, name="cls")[:]
+            nc.tensor.matmul(out=cls[0], lhsT=ones[:], rhs=bias_row[:], start=True, stop=True)
 
         def copy_bias():
-            nc.vector.tensor_copy(out=bias[:], in_=cls[0][:])
+            nc.vector.tensor_copy(out=bias[:], in_=cls[0])
 
         def warm_up(n):
             warm_ps = psum_agg.tile([P, FEATS], F32, name="agg")
@@ -201,7 +203,7 @@ def tile_gat_pb_kernel(tc, adj, h1, lin_w, lin_b, out_0, out_1, out_2):
 
         def transpose_x2(i):
             words = x2[i][:].bitcast(F32)
-            if i == ROW_TILES - 1:
+            if i in (5, 7):
                 x2_t[i] = psum_adj.tile([P, PASSES * HALVES, P], F32, name="adj_t")
             else:
                 x2_t[i] = psum_x2.tile([P, HALVES, P], F32, name="x2_t")
@@ -225,9 +227,12 @@ def tile_gat_pb_kernel(tc, adj, h1, lin_w, lin_b, out_0, out_1, out_2):
             )
 
         def classify(i):
-            cls[i] = psum_cls.tile([P, CLASSES], F32, name="cls")
+            if i in (5, 7):
+                cls[i] = psum_adj.tile([P, PASSES * HALVES, P], F32, name="adj_t")[:, 0, :]
+            else:
+                cls[i] = psum_cls.tile([P, CLASSES], F32, name="cls")[:]
             nc.tensor.matmul_mx(
-                out=cls[i][:],
+                out=cls[i],
                 lhsT=x2_codes[i][:].bitcast(FP8X4),
                 lhsT_scale=x2_scales[i][:],
                 rhs=w_codes[:].bitcast(FP8X4),
@@ -240,13 +245,18 @@ def tile_gat_pb_kernel(tc, adj, h1, lin_w, lin_b, out_0, out_1, out_2):
             return slice(i + 1 - STORE_GROUP, i + 1)
 
         def add_bias(i):
-            nc.vector.tensor_tensor(out=scores_sb[:, i, :], in0=cls[i][:], in1=bias[:], op=ALU.add)
+            nc.vector.tensor_tensor(out=scores_sb[:, i, :], in0=cls[i], in1=bias[:], op=ALU.add)
             if (i + 1) % STORE_GROUP == 0:
                 nc.sync.dma_start(out=scores_rows[:, group_of(i), :], in_=scores_sb[:, group_of(i), :])
 
         def negative_max(i):
             nc.vector.tensor_reduce(
                 out=neg_max[:, i : i + 1], in_=scores_sb[:, i, :], axis=AXIS.X, op=ALU.max, negate=True
+            )
+
+        def shift(i):
+            nc.scalar.activation(
+                out=shifted[:, i, :], in_=scores_sb[:, i, :], func=ACT.Identity, bias=neg_max[:, i : i + 1]
             )
 
         def sum_of_exp(i):
@@ -289,37 +299,39 @@ def tile_gat_pb_kernel(tc, adj, h1, lin_w, lin_b, out_0, out_1, out_2):
         def in_range(i):
             return 0 <= i < ROW_TILES
 
-        for s in range(-3, ROW_TILES + 7):
+        for s in range(-3, 6):
             if in_range(s + 1):
                 first_elu_negative(s + 1)
-            if in_range(s - 2):
+            if s < 99 and in_range(s - 2):
                 quantise_x2(s - 2)
-            if in_range(s - 4):
+            if s < 99 and in_range(s - 4):
                 negative_max(s - 4)
             if in_range(s):
                 second_elu(s)
-            if in_range(s - 7):
-                sum_of_exp(s - 7)
+            if s >= 99 and in_range(s - 2):
+                quantise_x2(s - 2)
+            if s >= 99 and in_range(s - 4):
+                negative_max(s - 4)
             if in_range(s + 2):
                 first_elu_exp(s + 2)
             if 3 <= s + 5 < ROW_TILES:
                 transpose_adj(s + 5)
             if in_range(s - 2):
                 classify(s - 2)
-            if in_range(s - 1):
+            if s < 99 and in_range(s - 1):
                 regroup_x2(s - 1)
             if in_range(s + 4):
                 quantise_adj(s + 4)
             if in_range(s + 1) and s + 1 < 4:
                 first_elu(s + 1)
-            if s == ROW_TILES:
-                first_elu(4)
             if s == 1:
                 spread_bias()
             if 1 <= s + 3 < ROW_TILES:
                 aggregate(s + 3)
             if in_range(s + 1):
                 second_elu_exp(s + 1)
+            if s >= 99 and in_range(s - 1):
+                regroup_x2(s - 1)
             if in_range(s):
                 transpose_x2(s)
             if s == -2:
@@ -329,35 +341,60 @@ def tile_gat_pb_kernel(tc, adj, h1, lin_w, lin_b, out_0, out_1, out_2):
                 copy_bias()
             if in_range(s - 2):
                 add_bias(s - 2)
-            if s == ROW_TILES + 4:
-                for i in range(4 + 1, ROW_TILES):
-                    first_elu(i)
             if 2 <= s + 5 < ROW_TILES:
                 regroup_adj(s + 5)
 
-        inverse_sum = keep.tile([P, ROW_TILES], F32)
-        neg_log_sum = keep.tile([P, ROW_TILES], F32)
+        first_elu_negative(7)
+        second_elu_exp(7)
+        first_elu(4)
+        second_elu(6)
+        quantise_x2(4)
+        transpose_x2(6)
+        classify(4)
+        regroup_x2(5)
+        second_elu(7)
+        transpose_x2(7)
+        quantise_x2(5)
+        add_bias(4)
+        classify(5)
+        negative_max(2)
+        regroup_x2(6)
+        quantise_x2(6)
+        negative_max(3)
+        add_bias(5)
+        classify(6)
+        negative_max(4)
+        regroup_x2(7)
+        for i in range(4): sum_of_exp(i)
+        for i in range(3): shift(i)
+        quantise_x2(7)
+        classify(7)
+        add_bias(6)
+        negative_max(5)
+        for i in range(4, 6): sum_of_exp(i)
+        negative_max(6)
+        sum_of_exp(6)
+        add_bias(7)
+        negative_max(7)
+        sum_of_exp(7)
+        first_elu(5)
         nc.vector.reciprocal(out=inverse_sum[:], in_=exp_sum[:])
-        for i in range(5, ROW_TILES):
-            nc.vector.tensor_scalar(
-                out=shifted[:, i, :], in0=scores_sb[:, i, :], scalar1=neg_max[:, i : i + 1], scalar2=None, op0=ALU.add
-            )
+        for i in range(6, 8): first_elu(i)
+
         nc.scalar.activation(out=neg_log_sum[:], in_=inverse_sum[:], func=ACT.Ln)
-        for i in range(5, ROW_TILES):
+        for i in (0, 1, 2,):
             nc.scalar.activation(
                 out=logp_sb[:, i, :], in_=shifted[:, i, :], func=ACT.Identity, bias=neg_log_sum[:, i : i + 1]
             )
-        for i in range(5):
-            nc.vector.tensor_scalar(
-                out=logp_sb[:, i, :],
-                in0=scores_sb[:, i, :],
-                scalar1=neg_max[:, i : i + 1],
-                scalar2=neg_log_sum[:, i : i + 1],
-                op0=ALU.add,
-                op1=ALU.add,
-            )
-            if i == 1:
-                nc.sync.dma_start(out=logp_rows[:, 0:2, :], in_=logp_sb[:, 0:2, :])
-            if i == 4:
-                nc.sync.dma_start(out=logp_rows[:, 2:5, :], in_=logp_sb[:, 2:5, :])
-        nc.sync.dma_start(out=logp_rows[:, 5:, :], in_=logp_sb[:, 5:, :])
+        for i in range(ROW_TILES):
+            if i not in (0, 1, 2,):
+                nc.vector.tensor_scalar(
+                    out=logp_sb[:, i, :],
+                    in0=scores_sb[:, i, :],
+                    scalar1=neg_max[:, i : i + 1],
+                    scalar2=neg_log_sum[:, i : i + 1],
+                    op0=ALU.add,
+                    op1=ALU.add,
+                )
+        for rows in (slice(3, 5), slice(0, 3), slice(5, 8)):
+            nc.sync.dma_start(out=logp_rows[:, rows, :], in_=logp_sb[:, rows, :])

@@ -210,6 +210,18 @@ def tile_gat_pb_kernel(tc, adj, h1, lin_w, lin_b, out_0, out_1, out_2):
             for u in range(HALVES):
                 nc.tensor.transpose(x2_t[i][:, u, :], words[:, u * P : (u + 1) * P], identity[:])
 
+            for j in range({5: 2}.get(i, 0)):
+                spare = psum_adj.tile([P, FEATS], F32, name="adj_t")
+                nc.tensor.matmul_mx(
+                    out=spare[:],
+                    lhsT=h1_codes[:, 0, :P].bitcast(FP8X4),
+                    lhsT_scale=h1_scales[:, 0, :P],
+                    rhs=h1_codes[:, 0, :].bitcast(FP8X4),
+                    rhs_scale=h1_scales[:, 0, :],
+                    start=True,
+                    stop=True,
+                )
+
         def regroup_x2(i):
             x2_grouped[i] = ring.tile([P, P * PACK], BF16, name="x2_grouped", align_bytes=64)
             nc.scalar.copy(

@@ -109,10 +109,12 @@ def tile_gat_pb_kernel(tc, adj, h1, lin_w, lin_b, out_0, out_1, out_2):
         def copy_bias():
             nc.vector.tensor_copy(out=bias[:], in_=cls[0])
 
-        def warm_up(n):
+        def warm_up(widths):
             warm_ps = psum_agg.tile([P, FEATS], F32, name="agg")
-            for j in range(n):
-                nc.tensor.matmul(out=warm_ps[:], lhsT=ones[:], rhs=zeros[:], start=True, stop=True)
+            for width in widths:
+                nc.tensor.matmul(
+                    out=warm_ps[:, :width], lhsT=ones[:], rhs=zeros[:, :width], start=True, stop=True
+                )
 
         def to_words(grouped):
             return grouped.rearrange("p (c i) t -> p c t i", i=RUN)
@@ -283,7 +285,7 @@ def tile_gat_pb_kernel(tc, adj, h1, lin_w, lin_b, out_0, out_1, out_2):
 
 
         on_vector, on_scalar = nc.vector.tensor_copy, nc.scalar.copy
-        warm_up(4)
+        warm_up((448, 512, 512, 512, 512))
         for h in range(2):
             regroup_h1_pass(h, 0, on_vector)
             regroup_h1_pass(h, 1, on_scalar)
@@ -294,7 +296,7 @@ def tile_gat_pb_kernel(tc, adj, h1, lin_w, lin_b, out_0, out_1, out_2):
         regroup_h1_pass(2, 0, on_vector)
         quantise_h1_pass(1, 1)
         transpose_adj(0)
-        warm_up(2)
+        warm_up((512, 512))
         regroup_adj(0)
         regroup_h1_pass(3, 0, on_vector)
         regroup_h1_pass(3, 1, on_vector)

@@ -32,7 +32,7 @@ def tile_gat_pb_kernel(tc, adj, h1, lin_w, lin_b, out_0, out_1, out_2):
     nc = tc.nc
 
     adj_rows = adj.rearrange("(p i) m -> p i m", i=ROW_TILES)
-    h1_rows = h1.rearrange("h (g p t) f -> h p g (t f)", g=PASSES, p=P, t=PACK)
+    h1_rows = h1.rearrange("h (c p e) f -> h p c (e f)", c=PASSES * HALVES, p=P, e=2)
     w_rows = lin_w.rearrange("(u p e) c -> p u (e c)", u=HALVES, e=2)
     logp_rows = out_0.rearrange("(p i) c -> p i c", i=ROW_TILES)
     emb1_rows = out_1.rearrange("(p i) c -> p i c", i=ROW_TILES)
@@ -66,7 +66,7 @@ def tile_gat_pb_kernel(tc, adj, h1, lin_w, lin_b, out_0, out_1, out_2):
 
         def load_h1(h):
             nc.sync.dma_start(
-                out=h1_raw[h][:].rearrange("p g t f -> p g (t f)"), in_=h1_rows[h]
+                out=h1_raw[h][:].rearrange("p g (u e) f -> p (g u) (e f)", e=2), in_=h1_rows[h]
             )
 
         load_h1(0)
@@ -145,10 +145,8 @@ def tile_gat_pb_kernel(tc, adj, h1, lin_w, lin_b, out_0, out_1, out_2):
         def transpose_adj(i):
             words = adj_sb[i][:].bitcast(F32)
             adj_t[i] = psum_adj.tile([P, PASSES * HALVES, P], F32, name="adj_t")
-            for g in range(PASSES):
-                for u in range(HALVES):
-                    half = words[:, HALVES * g * P + u : HALVES * (g + 1) * P : HALVES]
-                    nc.tensor.transpose(adj_t[i][:, HALVES * g + u, :], half, identity[:])
+            for c in range(PASSES * HALVES):
+                nc.tensor.transpose(adj_t[i][:, c, :], words[:, c * P : (c + 1) * P], identity[:])
 
         def regroup_adj(i):
             adj_grouped[i] = ring.tile([P, PASSES * P * PACK], BF16, name="adj_grouped", align_bytes=64)

from contextlib import ExitStack

import concourse.mybir as mybir
from concourse.masks import make_identity

F32 = mybir.dt.float32
BF16 = mybir.dt.bfloat16
U32 = mybir.dt.uint32
U8 = mybir.dt.uint8
FP8X4 = mybir.dt.float8_e4m3fn_x4
ACT = mybir.ActivationFunctionType
ALU = mybir.AluOpType
AXIS = mybir.AxisListType

P = 128
PACK = 4
NODES = 1024
HEADS = 4
HID = 128
FEATS = HEADS * HID
CLASSES = 128
ROW_TILES = NODES // P
PASSES = NODES // (P * PACK)
HALVES = 2
STORE_GROUP = 4
RUN = 4

FLOPS = 2 * NODES * NODES * FEATS + 2 * NODES * FEATS * CLASSES


def tile_gat_pb_kernel(tc, adj, h1, lin_w, lin_b, out_0, out_1, out_2):
    nc = tc.nc

    adj_rows = adj.rearrange("(p i) m -> p i m", i=ROW_TILES)
    h1_rows = h1.rearrange("h (c p e) f -> h p c (e f)", c=PASSES * HALVES, p=P, e=2)
    w_rows = lin_w.rearrange("(u p e) c -> p u (e c)", u=HALVES, e=2)
    logp_rows = out_0.rearrange("(p i) c -> p i c", i=ROW_TILES)
    emb1_rows = out_1.rearrange("(p i) c -> p i c", i=ROW_TILES)
    scores_rows = out_2.rearrange("(p i) c -> p i c", i=ROW_TILES)

    with ExitStack() as ctx:
        keep = ctx.enter_context(tc.tile_pool(name="keep", bufs=1))
        inputs = ctx.enter_context(tc.tile_pool(name="inputs", bufs=1))
        ring = ctx.enter_context(tc.tile_pool(name="ring", bufs=4))
        psum_adj = ctx.enter_context(tc.psum_pool(name="psum_adj", bufs=2))
        psum_agg = ctx.enter_context(tc.psum_pool(name="psum_agg", bufs=4))
        psum_x2 = ctx.enter_context(tc.psum_pool(name="psum_x2", bufs=1))
        psum_cls = ctx.enter_context(tc.psum_pool(name="psum_cls", bufs=1))
        ctx.enter_context(tc.manual_schedule())

        identity = keep.tile([P, P], F32)
        make_identity(nc, identity[:])
        ones = keep.tile([P, P], BF16)
        nc.vector.memset(ones[:], 1.0)
        zeros = keep.tile([P, FEATS], BF16)
        nc.gpsimd.memset(zeros[:], 0.0)
        bias_row = keep.tile([P, CLASSES], BF16)
        nc.vector.memset(bias_row[:], 0.0)

        adj_sb = [inputs.tile([P, NODES], BF16, name="adj_sb%d" % i) for i in range(ROW_TILES)]
        h1_raw = [inputs.tile([P, PASSES, PACK, HID], BF16, name="h1_raw%d" % h) for h in range(HEADS)]
        w_raw = inputs.tile([P, PACK, CLASSES], BF16)

        def load_adj(i):
            nc.sync.dma_start(out=adj_sb[i][:], in_=adj_rows[:, i, :])

        def load_h1(h):
            nc.sync.dma_start(
                out=h1_raw[h][:].rearrange("p g (u e) f -> p (g u) (e f)", e=2), in_=h1_rows[h]
            )

        load_h1(0)
        load_h1(1)
        load_h1(2)
        load_adj(0)
        load_h1(3)
        load_adj(1)
        load_adj(2)
        load_adj(3)
        nc.sync.dma_start(out=w_raw[:].rearrange("p (u e) c -> p u (e c)", e=2), in_=w_rows)
        for i in range(4, ROW_TILES):
            load_adj(i)
            if i == 5:
                nc.sync.dma_start(out=bias_row[0:1, :], in_=lin_b.unsqueeze(0))

        h1_grouped = keep.tile([P, PASSES, FEATS, PACK], BF16, align_bytes=64)
        h1_codes = keep.tile([P, PASSES, FEATS], U32, align_bytes=64)
        h1_scales = keep.tile([P, PASSES, FEATS], U8, align_bytes=64)
        w_grouped = keep.tile([P, CLASSES, PACK], BF16, align_bytes=64)
        w_codes = keep.tile([P, CLASSES], U32, align_bytes=64)
        w_scales = keep.tile([P, CLASSES], U8, align_bytes=64)
        bias = keep.tile([P, CLASSES], F32)
        scores_sb = keep.tile([P, ROW_TILES, CLASSES], F32)
        logp_sb = keep.tile([P, ROW_TILES, CLASSES], F32)
        exp_shifted = keep.tile([P, ROW_TILES, CLASSES], F32)
        shifted = keep.tile([P, ROW_TILES, CLASSES], F32)
        neg_max = keep.tile([P, ROW_TILES], F32)
        exp_sum = keep.tile([P, ROW_TILES], F32)
        inverse_sum = keep.tile([P, ROW_TILES], F32)
        neg_log_sum = keep.tile([P, ROW_TILES], F32)

        adj_t, adj_grouped, adj_codes, adj_scales = {}, {}, {}, {}
        agg, exp_v, neg, emb1, exp_neg, x2, x2_t, x2_grouped, x2_codes, x2_scales, cls = {}, {}, {}, {}, {}, {}, {}, {}, {}, {}, {}

        def spread_bias():
            cls[0] = psum_cls.tile([P, CLASSES], F32, name="cls")[:]
            nc.tensor.matmul(out=cls[0], lhsT=ones[:], rhs=bias_row[:], start=True, stop=True)

        def copy_bias():
            nc.vector.tensor_copy(out=bias[:], in_=cls[0])

        def warm_up(widths):
            warm_ps = psum_agg.tile([P, FEATS], F32, name="agg")
            for width in widths:
                nc.tensor.matmul(
                    out=warm_ps[:, :width], lhsT=ones[:], rhs=zeros[:, :width], start=True, stop=True
                )

        def to_words(grouped):
            return grouped.rearrange("p (c i) t -> p c t i", i=RUN)

        def from_rows(raw):
            return raw.rearrange("p t (c i) -> p c t i", i=RUN)

        def regroup_h1_pass(h, g, copy):
            cols = slice(h * HID, (h + 1) * HID)
            copy(out=to_words(h1_grouped[:, g, cols, :]), in_=from_rows(h1_raw[h][:, g]))

        def quantise_h1_pass(h, g):
            cols = slice(h * HID, (h + 1) * HID)
            nc.vector.quantize_mx(
                out=h1_codes[:, g, cols].bitcast(FP8X4),
                scales=h1_scales[:, g, cols],
                in_=h1_grouped[:, g, cols, :].rearrange("p f t -> p (f t)"),
            )

        def prepare_classifier():
            nc.vector.tensor_copy(out=to_words(w_grouped[:]), in_=from_rows(w_raw[:]))

        def quantise_w():
            nc.vector.quantize_mx(
                out=w_codes[:].bitcast(FP8X4), scales=w_scales[:], in_=w_grouped[:].rearrange("p c t -> p (c t)")
            )

        def transpose_adj(i):
            words = adj_sb[i][:].bitcast(F32)
            adj_t[i] = psum_adj.tile([P, PASSES * HALVES, P], F32, name="adj_t")
            for c in range(PASSES * HALVES):
                nc.tensor.transpose(adj_t[i][:, c, :], words[:, c * P : (c + 1) * P], identity[:])

        def regroup_adj(i):
            adj_grouped[i] = ring.tile([P, PASSES * P * PACK], BF16, name="adj_grouped", align_bytes=64)
            nc.scalar.copy(
                out=adj_grouped[i][:].bitcast(F32).rearrange("p (g n u) -> p g n u", g=PASSES, u=HALVES),
                in_=adj_t[i][:].rearrange("p (g u) n -> p g n u", u=HALVES),
            )

        def quantise_adj(i):
            adj_codes[i] = ring.tile([P, PASSES * P], U32, name="adj_codes", align_bytes=64)
            adj_scales[i] = ring.tile([P, PASSES * P], U8, name="adj_scales", align_bytes=64)
            nc.vector.quantize_mx(
                out=adj_codes[i][:].bitcast(FP8X4), scales=adj_scales[i][:], in_=adj_grouped[i][:]
            )

        def aggregate(i):
            agg[i] = psum_agg.tile([P, FEATS], F32, name="agg")
            for g, start, stop in ((0, True, False), (1, False, True)):
                rows = slice(g * P, (g + 1) * P)
                nc.tensor.matmul_mx(
                    out=agg[i][:],
                    lhsT=adj_codes[i][:, rows].bitcast(FP8X4),
                    lhsT_scale=adj_scales[i][:, rows],
                    rhs=h1_codes[:, g, :].bitcast(FP8X4),
                    rhs_scale=h1_scales[:, g, :],
                    start=start,
                    stop=stop,
                )

        def first_elu_exp(i):
            exp_v[i] = ring.tile([P, FEATS], F32, name="exp_v")
            nc.scalar.activation(out=exp_v[i][:], in_=agg[i][:], func=ACT.Exp)

        def first_elu_negative(i):
            neg[i] = ring.tile([P, FEATS], F32, name="neg")
            nc.vector.tensor_scalar(
                out=neg[i][:], in0=exp_v[i][:], scalar1=1.0, scalar2=-1.0, op0=ALU.min, op1=ALU.add
            )

        def first_elu(i):
            emb1[i] = ring.tile([P, FEATS], F32, name="emb1")
            nc.vector.tensor_tensor(out=emb1[i][:], in0=agg[i][:], in1=neg[i][:], op=ALU.max)
            nc.sync.dma_start(out=emb1_rows[:, i, :], in_=emb1[i][:])

        def second_elu_exp(i):
            exp_neg[i] = ring.tile([P, FEATS], F32, name="exp_neg")
            nc.scalar.activation(out=exp_neg[i][:], in_=neg[i][:], func=ACT.Exp)

        def second_elu(i):
            x2[i] = ring.tile([P, FEATS], BF16, name="x2")
            nc.vector.scalar_tensor_tensor(
                out=x2[i][:], in0=exp_neg[i][:], scalar=-1.0, in1=agg[i][:], op0=ALU.add, op1=ALU.max
            )

        def transpose_x2(i):
            words = x2[i][:].bitcast(F32)
            if i in (5, 7):
                x2_t[i] = psum_adj.tile([P, PASSES * HALVES, P], F32, name="adj_t")
            else:
                x2_t[i] = psum_x2.tile([P, HALVES, P], F32, name="x2_t")
            for u in range(HALVES):
                nc.tensor.transpose(x2_t[i][:, u, :], words[:, u * P : (u + 1) * P], identity[:])

            for j in range({5: 2}.get(i, 0)):
                spare = psum_adj.tile([P, FEATS], F32, name="adj_t")
                nc.tensor.matmul_mx(
                    out=spare[:],
                    lhsT=h1_codes[:, 0, :P].bitcast(FP8X4),
                    lhsT_scale=h1_scales[:, 0, :P],
                    rhs=h1_codes[:, 0, :].bitcast(FP8X4),
                    rhs_scale=h1_scales[:, 0, :],
                    start=True,
                    stop=True,
                )

        def regroup_x2(i):
            x2_grouped[i] = ring.tile([P, P * PACK], BF16, name="x2_grouped", align_bytes=64)
            nc.scalar.copy(
                out=x2_grouped[i][:].bitcast(F32).rearrange("p (n u) -> p n u", u=HALVES),
                in_=x2_t[i][:, :HALVES, :].rearrange("p u n -> p n u"),
            )

        def quantise_x2(i):
            x2_codes[i] = ring.tile([P, P], U32, name="x2_codes", align_bytes=64)
            x2_scales[i] = ring.tile([P, P], U8, name="x2_scales", align_bytes=64)
            nc.vector.quantize_mx(
                out=x2_codes[i][:].bitcast(FP8X4),
                scales=x2_scales[i][:],
                in_=x2_grouped[i][:],
            )

        def classify(i):
            if i in (5, 7):
                cls[i] = psum_adj.tile([P, PASSES * HALVES, P], F32, name="adj_t")[:, 0, :]
            else:
                cls[i] = psum_cls.tile([P, CLASSES], F32, name="cls")[:]
            nc.tensor.matmul_mx(
                out=cls[i],
                lhsT=x2_codes[i][:].bitcast(FP8X4),
                lhsT_scale=x2_scales[i][:],
                rhs=w_codes[:].bitcast(FP8X4),
                rhs_scale=w_scales[:],
                start=True,
                stop=True,
            )

        def group_of(i):
            return slice(i + 1 - STORE_GROUP, i + 1)

        def add_bias(i):
            nc.vector.tensor_tensor(out=scores_sb[:, i, :], in0=cls[i], in1=bias[:], op=ALU.add)
            if (i + 1) % STORE_GROUP == 0:
                nc.sync.dma_start(out=scores_rows[:, group_of(i), :], in_=scores_sb[:, group_of(i), :])

        def negative_max(i):
            nc.vector.tensor_reduce(
                out=neg_max[:, i : i + 1], in_=scores_sb[:, i, :], axis=AXIS.X, op=ALU.max, negate=True
            )

        def shift(i):
            nc.scalar.activation(
                out=shifted[:, i, :], in_=scores_sb[:, i, :], func=ACT.Identity, bias=neg_max[:, i : i + 1]
            )

        def sum_of_exp(i):
            nc.scalar.activation(
                out=exp_shifted[:, i, :],
                in_=scores_sb[:, i, :],
                func=ACT.Exp,
                bias=neg_max[:, i : i + 1],
                scale=1.0,
                accum_out=exp_sum[:, i : i + 1],
            )


        on_vector, on_scalar = nc.vector.tensor_copy, nc.scalar.copy
        warm_up((448, 512, 512, 512, 512))
        for h in range(2):
            regroup_h1_pass(h, 0, on_vector)
            regroup_h1_pass(h, 1, on_scalar)
        regroup_h1_pass(2, 1, on_scalar)
        quantise_h1_pass(0, 0)
        quantise_h1_pass(1, 0)
        quantise_h1_pass(0, 1)
        regroup_h1_pass(2, 0, on_vector)
        quantise_h1_pass(1, 1)
        transpose_adj(0)
        warm_up((512, 512))
        regroup_adj(0)
        regroup_h1_pass(3, 0, on_vector)
        regroup_h1_pass(3, 1, on_vector)
        quantise_h1_pass(2, 0)
        quantise_h1_pass(3, 0)
        quantise_adj(0)
        quantise_h1_pass(2, 1)
        quantise_h1_pass(3, 1)
        transpose_adj(1)
        regroup_adj(1)
        transpose_adj(2)
        aggregate(0)

        def in_range(i):
            return 0 <= i < ROW_TILES

        for s in range(-3, 6):
            if in_range(s + 1):
                first_elu_negative(s + 1)
            if s < 99 and in_range(s - 2):
                quantise_x2(s - 2)
            if s < 99 and in_range(s - 4):
                negative_max(s - 4)
            if in_range(s):
                second_elu(s)
            if s >= 99 and in_range(s - 2):
                quantise_x2(s - 2)
            if s >= 99 and in_range(s - 4):
                negative_max(s - 4)
            if in_range(s + 2):
                first_elu_exp(s + 2)
            if 3 <= s + 5 < ROW_TILES:
                transpose_adj(s + 5)
            if in_range(s - 2):
                classify(s - 2)
            if s < 99 and in_range(s - 1):
                regroup_x2(s - 1)
            if in_range(s + 4):
                quantise_adj(s + 4)
            if in_range(s + 1) and s + 1 < 4:
                first_elu(s + 1)
            if s == 1:
                spread_bias()
            if 1 <= s + 3 < ROW_TILES:
                aggregate(s + 3)
            if in_range(s + 1):
                second_elu_exp(s + 1)
            if s >= 99 and in_range(s - 1):
                regroup_x2(s - 1)
            if in_range(s):
                transpose_x2(s)
            if s == -2:
                prepare_classifier()
                quantise_w()
            if s == 1:
                copy_bias()
            if in_range(s - 2):
                add_bias(s - 2)
            if 2 <= s + 5 < ROW_TILES:
                regroup_adj(s + 5)

        first_elu_negative(7)
        second_elu_exp(7)
        first_elu(4)
        second_elu(6)
        quantise_x2(4)
        transpose_x2(6)
        classify(4)
        regroup_x2(5)
        second_elu(7)
        transpose_x2(7)
        quantise_x2(5)
        add_bias(4)
        classify(5)
        negative_max(2)
        regroup_x2(6)
        quantise_x2(6)
        negative_max(3)
        add_bias(5)
        classify(6)
        negative_max(4)
        regroup_x2(7)
        for i in range(4): sum_of_exp(i)
        for i in range(3): shift(i)
        quantise_x2(7)
        classify(7)
        add_bias(6)
        negative_max(5)
        for i in range(4, 6): sum_of_exp(i)
        negative_max(6)
        sum_of_exp(6)
        add_bias(7)
        negative_max(7)
        sum_of_exp(7)
        first_elu(5)
        nc.vector.reciprocal(out=inverse_sum[:], in_=exp_sum[:])
        for i in range(6, 8): first_elu(i)

        nc.scalar.activation(out=neg_log_sum[:], in_=inverse_sum[:], func=ACT.Ln)
        for i in (0, 1, 2,):
            nc.scalar.activation(
                out=logp_sb[:, i, :], in_=shifted[:, i, :], func=ACT.Identity, bias=neg_log_sum[:, i : i + 1]
            )
        for i in range(ROW_TILES):
            if i not in (0, 1, 2,):
                nc.vector.tensor_scalar(
                    out=logp_sb[:, i, :],
                    in0=scores_sb[:, i, :],
                    scalar1=neg_max[:, i : i + 1],
                    scalar2=neg_log_sum[:, i : i + 1],
                    op0=ALU.add,
                    op1=ALU.add,
                )
        for rows in (slice(3, 5), slice(0, 3), slice(5, 8)):
            nc.sync.dma_start(out=logp_rows[:, rows, :], in_=logp_sb[:, rows, :])
